import numpy as np
import ml_dtypes


def mxq(x, axis, fmt="e4m3"):
    dtype, down = {"e4m3": (ml_dtypes.float8_e4m3fn, 7), "e5m2": (ml_dtypes.float8_e5m2, 14)}[fmt]
    v = np.moveaxis(np.asarray(x, np.float32).astype(ml_dtypes.bfloat16).astype(np.float64), axis, -1)
    blocks = v.reshape(v.shape[:-1] + (-1, 32))
    amax = np.abs(blocks).max(-1, keepdims=True)
    byte = np.maximum(np.where(amax > 0, np.frexp(amax)[1] - 1 + 127, 0) - down, 1)
    scale = np.exp2(byte - 127.0)
    codes = (blocks / scale).astype(np.float32).astype(dtype).astype(np.float64)
    return np.moveaxis((codes * scale).reshape(v.shape), -1, axis)


WIDE = False


def mx_kscale(k):
    if not WIDE:
        return np.ones(k)
    levels = np.array([10, -10, 5, -5, 0])
    a = np.random.permutation(np.resize(levels, k // 512 * 4)).reshape(k // 512, 4)
    idx = np.arange(k)
    return np.exp2(a[idx // 512, idx % 128 // 32])


BF16 = ml_dtypes.bfloat16


def bf(x):
    return np.asarray(x, np.float32).astype(BF16)


def f64(x):
    return np.asarray(x).astype(np.float64)


E2M1 = np.array([0.0, 0.5, 1.0, 1.5, 2.0, 3.0, 4.0, 6.0, -0.0, -0.5, -1.0, -1.5, -2.0, -3.0, -4.0, -6.0])


def pack_weight(w, fmt):
    k, n = w.shape
    w = f64(bf(w)).reshape(k // 32, 32, n)
    amax = np.abs(w).max(1)
    if fmt == "e4m3":
        byte = np.frexp(amax)[1] - 1 + 127 - 7
    else:
        mant, ex = np.frexp(amax / 6.0)
        byte = np.where(mant > 0.5, ex, ex - 1) + 127
    byte = np.clip(np.where(amax > 0, byte, 1), 1, 254)
    scaled = (w * np.exp2(127.0 - byte)[:, None, :]).reshape(k, n).astype(np.float32)
    by_word = np.ascontiguousarray(scaled.reshape(k // 512, 128, 4, n).transpose(0, 1, 3, 2))
    if fmt == "e4m3":
        words = by_word.astype(ml_dtypes.float8_e4m3fn).view(np.uint8)
    else:
        c = by_word.astype(ml_dtypes.float4_e2m1fn).view(np.uint8) & 0xF
        words = c[..., 0::2] | (c[..., 1::2] << 4)
    return np.ascontiguousarray(words), np.ascontiguousarray(byte.astype(np.uint8).reshape(k // 512, 16, n))


def unpack_weight(words, scales, fmt):
    g, p, n, _ = words.shape
    if fmt == "e4m3":
        vals = np.ascontiguousarray(words).view(ml_dtypes.float8_e4m3fn).astype(np.float64)
    else:
        nib = np.empty((g, p, n, 4), np.uint8)
        nib[..., 0::2] = words & 0xF
        nib[..., 1::2] = words >> 4
        vals = E2M1[nib]
    vals = vals * np.repeat(np.exp2(scales.astype(np.float64) - 127.0), 8, axis=1)[..., None]
    return vals.transpose(0, 1, 3, 2).reshape(g * 512, n)


B, F, H1, E, N, P, L, C, S = 512, 2048, 16384, 512, 32, 8, 100, 16, 100
EPS = 1e-5


def layernorm(x, g, b):
    mu = x.mean(axis=-1, keepdims=True)
    var = x.var(axis=-1, keepdims=True)
    return (x - mu) / np.sqrt(var + EPS) * g + b


def setup_inputs():
    rn = np.random.standard_normal
    s = mx_kscale(H1)
    t = mx_kscale(E)
    h1 = bf(np.maximum(rn((B, H1)), 0.0) * s)
    W2_words, W2_scales = pack_weight(rn((H1, E)) / np.sqrt(H1) / s[:, None], "e4m3")
    return {"h1": h1,
            "W2_words": W2_words,
            "W2_scales": W2_scales,
            "b2": bf(rn(E) * 0.3),
            "ln_g": bf((1.0 + 0.2 * rn(E)) * t),
            "ln_b": bf(0.3 * rn(E) * t),
            "pc_W": bf(rn((N, E, P)) / np.sqrt(E) / t[None, :, None]),
            "pc_b": bf(0.3 * rn((N, P))),
            "pc_g": bf(1.0 + 0.2 * rn((N, P))),
            "pc_beta": bf(0.3 * rn((N, P)))}


def reference(h1, W2_words, W2_scales, b2, ln_g, ln_b, pc_W, pc_b, pc_g, pc_beta):
    z = np.maximum((mxq(f64(h1), 1, "e4m3") @ unpack_weight(W2_words, W2_scales, "e4m3")) + f64(b2), 0.0)
    h = layernorm(z, f64(ln_g), f64(ln_b))
    w = mxq(f64(pc_W), 1, "e4m3").transpose(1, 0, 2).reshape(E, N * P)
    prim = (mxq(h, 1, "e4m3") @ w).reshape(B, N, P) + f64(pc_b)[None]
    return layernorm(prim, f64(pc_g)[None], f64(pc_beta)[None])

@@ -1,0 +1,374 @@
+from contextlib import ExitStack
+
+import concourse.mybir as mybir
+from concourse.masks import make_identity
+
+F32 = mybir.dt.float32
+BF16 = mybir.dt.bfloat16
+I32 = mybir.dt.int32
+U32 = mybir.dt.uint32
+U8 = mybir.dt.uint8
+FP8X4 = mybir.dt.float8_e4m3fn_x4
+ALU = mybir.AluOpType
+ACT = mybir.ActivationFunctionType
+AX = mybir.AxisListType
+
+P = 128
+PACK = 4
+K_PASS = P * PACK
+BATCH = 512
+HIDDEN = 16384
+EMBED = 512
+CAPSULES = 32
+CAP_DIM = 8
+CAP_OUT = CAPSULES * CAP_DIM
+EPS = 1e-5
+
+B_TILES = BATCH // P
+PASSES = HIDDEN // K_PASS
+CHUNK_PASSES = 8
+CHUNKS = PASSES // CHUNK_PASSES
+CHUNK_K = CHUNK_PASSES * K_PASS
+PASS_WORDS = K_PASS // 2
+BANK_PASSES = 2
+QUARTER_PASSES = 2
+PLANES = 4
+LOADS_AHEAD = 4
+
+FLOPS = 2 * BATCH * HIDDEN * EMBED + 2 * BATCH * EMBED * CAP_OUT
+
+AT_B2 = 0
+AT_LN_G = EMBED
+AT_LN_B = 2 * EMBED
+AT_PC_B = 3 * EMBED
+AT_PC_G = 3 * EMBED + CAP_OUT
+AT_PC_BETA = 3 * EMBED + 2 * CAP_OUT
+ROW_WIDTH = 3 * EMBED + 3 * CAP_OUT
+
+
+def tile_hotpatchcapsmodel_pa_k_kernel(
+    tc, h1, W2_words, W2_scales, b2, ln_g, ln_b, pc_W, pc_b, pc_g, pc_beta, out
+):
+    nc = tc.nc
+    rounds = [(chunk, bt) for chunk in range(CHUNKS) for bt in range(B_TILES)]
+    n_rounds = len(rounds)
+
+    with ExitStack() as ctx:
+        const = ctx.enter_context(tc.tile_pool(name="const", bufs=1))
+        raw_pool = ctx.enter_context(tc.tile_pool(name="raw", bufs=6))
+        stage = ctx.enter_context(tc.tile_pool(name="stage", bufs=2))
+        codes_pool = ctx.enter_context(tc.tile_pool(name="codes", bufs=3))
+        work = ctx.enter_context(tc.tile_pool(name="work", bufs=2))
+        small = ctx.enter_context(tc.tile_pool(name="small", bufs=2))
+        flip_psum = ctx.enter_context(tc.psum_pool(name="flip", bufs=4))
+        acc_psum = ctx.enter_context(tc.psum_pool(name="acc", bufs=1))
+
+        vec_row = const.tile([P, ROW_WIDTH], BF16)
+        nc.vector.memset(vec_row[:], 0.0)
+        w2_planes = const.tile([P, PASSES // PLANES, EMBED], U8, align_bytes=64)
+        nc.vector.memset(w2_planes[:].bitcast(I32), 0)
+        ones = const.tile([P, P], BF16)
+        nc.vector.memset(ones[:], 1.0)
+        eps_col = const.tile([P, 1], F32)
+        nc.vector.memset(eps_col[:], EPS)
+        table_warm = const.tile([P, 1], F32)
+        nc.scalar.activation(out=table_warm[:], in_=eps_col[:], func=ACT.Sqrt)
+        ident_f32 = const.tile([P, P], F32)
+        make_identity(nc, ident_f32[:])
+        ident_bf = const.tile([P, P], BF16)
+        make_identity(nc, ident_bf[:])
+        w2_codes = const.tile([P, PASSES, EMBED], U32, align_bytes=64)
+
+        pcw_raw = const.tile([P, P * CAP_DIM], BF16)
+        nc.scalar.dma_start(out=pcw_raw[:], in_=pc_W.rearrange("n (a e) p -> (n a) (e p)", e=P))
+        for vec, at in ((b2, AT_B2), (ln_g, AT_LN_G), (ln_b, AT_LN_B)):
+            nc.scalar.dma_start(
+                out=vec_row[0:1, at : at + EMBED], in_=vec.rearrange("(o e) -> o e", o=1)
+            )
+        for vec, at in ((pc_b, AT_PC_B), (pc_g, AT_PC_G), (pc_beta, AT_PC_BETA)):
+            nc.scalar.dma_start(
+                out=vec_row[0:1, at : at + CAP_OUT], in_=vec.rearrange("(o n) p -> o (n p)", o=1)
+            )
+
+        raw_tiles = {}
+        sorted_tiles = {}
+        grouped_tiles = {}
+        code_tiles = {}
+        acc = {}
+
+        def load_h1(r):
+            chunk, bt = rounds[r]
+            raw = raw_pool.tile([P, CHUNK_K], BF16, name="raw")
+            nc.sync.dma_start(
+                out=raw[:],
+                in_=h1[bt * P : (bt + 1) * P, chunk * CHUNK_K : (chunk + 1) * CHUNK_K],
+            )
+            raw_tiles[r] = raw
+
+        def load_w2_scales():
+            for quadrant in range(4):
+                for plane in range(PLANES):
+                    first = 32 * quadrant + 4 * plane
+                    nc.sync.dma_start(
+                        out=w2_planes[first : first + 4, :, :].bitcast(I32),
+                        in_=W2_scales[plane:PASSES:PLANES, 4 * quadrant : 4 * quadrant + 4, :]
+                        .rearrange("s r n -> r s n")
+                        .bitcast(I32),
+                    )
+
+        def load_w2_quarter(q):
+            passes = slice(q * QUARTER_PASSES, (q + 1) * QUARTER_PASSES)
+            nc.sync.dma_start(
+                out=w2_codes[:, passes, :].bitcast(I32),
+                in_=W2_words[passes].rearrange("g p n t -> p g (n t)").bitcast(I32),
+            )
+
+        def sort_words(r):
+            words = raw_tiles[r][:].bitcast(F32)
+            sorted_words = stage.tile([P, CHUNK_PASSES, 2, P], F32, name="sorted_words")
+            nc.vector.tensor_copy(
+                out=sorted_words[:],
+                in_=words.rearrange("b (g j u) -> b g u j", g=CHUNK_PASSES, u=2),
+            )
+            sorted_tiles[r] = sorted_words
+
+        def transpose_round(r):
+            sorted_words = sorted_tiles[r]
+            grouped = stage.tile([P, CHUNK_K], BF16, name="grouped", align_bytes=64)
+            grouped_words = grouped[:].bitcast(F32).rearrange(
+                "p (g b u) -> p g b u", g=CHUNK_PASSES, u=2
+            )
+            for first in range(0, CHUNK_PASSES, BANK_PASSES):
+                bank = flip_psum.tile([P, BANK_PASSES, 2, P], F32, name="bank", tag="flip")
+                for i in range(BANK_PASSES):
+                    for u in range(2):
+                        nc.tensor.transpose(
+                            bank[:, i, u, :], sorted_words[:, first + i, u, :], ident_f32[:]
+                        )
+                nc.scalar.copy(
+                    out=grouped_words[:, first : first + BANK_PASSES],
+                    in_=bank[:].rearrange("p g u b -> p g b u"),
+                )
+            grouped_tiles[r] = grouped
+
+        def quantise_round(r):
+            grouped = grouped_tiles[r]
+            codes = codes_pool.tile([P, CHUNK_PASSES * P], U32, name="codes", align_bytes=64)
+            scales = codes_pool.tile([P, CHUNK_PASSES * P], U8, name="scales", align_bytes=64)
+            half = CHUNK_PASSES * P // 2
+            for lo in (0, half):
+                nc.vector.quantize_mx(
+                    out=codes[:, lo : lo + half].bitcast(FP8X4),
+                    scales=scales[:, lo : lo + half],
+                    in_=grouped[:, PACK * lo : PACK * (lo + half)],
+                )
+            code_tiles[r] = (codes, scales)
+
+        def multiply_round(r):
+            chunk, bt = rounds[r]
+            codes, scales = code_tiles[r]
+            if chunk == 0:
+                acc[bt] = acc_psum.tile([P, EMBED], F32, name="acc%d" % bt)
+            for i in range(CHUNK_PASSES):
+                g = chunk * CHUNK_PASSES + i
+                cols = slice(i * P, (i + 1) * P)
+                nc.tensor.matmul_mx(
+                    out=acc[bt][:],
+                    lhsT=codes[:, cols].bitcast(FP8X4),
+                    lhsT_scale=scales[:, cols],
+                    rhs=w2_codes[:, g, :].bitcast(FP8X4),
+                    rhs_scale=w2_planes[4 * (g % PLANES) : P, g // PLANES, :],
+                    start=(g == 0),
+                    stop=(g == PASSES - 1),
+                )
+
+        load_h1(0)
+        load_h1(1)
+        load_w2_scales()
+        for q in range(CHUNK_PASSES // QUARTER_PASSES):
+            load_w2_quarter(q)
+        next_quarter = CHUNK_PASSES // QUARTER_PASSES
+        for r in range(2, LOADS_AHEAD):
+            load_h1(r)
+            load_w2_quarter(next_quarter)
+            next_quarter += 1
+
+        sort_words(0)
+        sort_words(1)
+        transpose_round(0)
+        quantise_round(0)
+
+        spread = const.tile([P, ROW_WIDTH], F32)
+        for lo in range(0, ROW_WIDTH, EMBED):
+            width = min(EMBED, ROW_WIDTH - lo)
+            rep = flip_psum.tile([P, width], F32, name="rep", tag="flip")
+            nc.tensor.matmul(
+                out=rep[:], lhsT=ones[:], rhs=vec_row[:, lo : lo + width], start=True, stop=True
+            )
+            nc.scalar.copy(out=spread[:, lo : lo + width], in_=rep[:])
+
+        pcw_sorted = const.tile([P, CAP_DIM, P], BF16)
+        nc.vector.tensor_copy(
+            out=pcw_sorted[:], in_=pcw_raw[:].rearrange("q (e p) -> q p e", p=CAP_DIM)
+        )
+        pcw_flip = flip_psum.tile([P, CAP_DIM, P], BF16, name="pcw_flip", tag="flip")
+        for p in range(CAP_DIM):
+            nc.tensor.transpose(pcw_flip[:, p, :], pcw_sorted[:, p, :], ident_bf[:])
+        pcw_grouped = const.tile([P, CAPSULES, CAP_DIM, PACK], BF16, align_bytes=64)
+        nc.vector.tensor_copy(
+            out=pcw_grouped[:], in_=pcw_flip[:].rearrange("e p (n a) -> e n p a", a=PACK)
+        )
+        pcw_codes = const.tile([P, CAP_OUT], U32, align_bytes=64)
+        pcw_scales = const.tile([P, CAP_OUT], U8, align_bytes=64)
+        nc.vector.quantize_mx(
+            out=pcw_codes[:].bitcast(FP8X4),
+            scales=pcw_scales[:],
+            in_=pcw_grouped[:].rearrange("e n p a -> e (n p a)"),
+        )
+
+        h_tiles = {}
+        h_code_tiles = {}
+
+        def norm_embedding(bt):
+            biased = work.tile([P, EMBED], F32, name="biased")
+            nc.vector.tensor_tensor(
+                out=biased[:], in0=acc[bt][:], in1=spread[:, AT_B2 : AT_B2 + EMBED], op=ALU.add
+            )
+            z = work.tile([P, EMBED], F32, name="z")
+            z_sum = small.tile([P, 1], F32, name="z_sum")
+            nc.scalar.activation(out=z[:], in_=biased[:], func=ACT.Relu, accum_out=z_sum[:])
+            neg_mean = small.tile([P, 1], F32, name="neg_mean")
+            nc.vector.tensor_scalar_mul(out=neg_mean[:], in0=z_sum[:], scalar1=-1.0 / EMBED)
+            squares = work.tile([P, EMBED], F32, name="squares")
+            sq_sum = small.tile([P, 1], F32, name="sq_sum")
+            nc.scalar.activation(
+                out=squares[:], in_=z[:], func=ACT.Square, bias=neg_mean[:], accum_out=sq_sum[:]
+            )
+            gained = work.tile([P, EMBED], F32, name="gained")
+            nc.vector.scalar_tensor_tensor(
+                out=gained[:],
+                in0=z[:],
+                scalar=neg_mean[:],
+                in1=spread[:, AT_LN_G : AT_LN_G + EMBED],
+                op0=ALU.add,
+                op1=ALU.mult,
+            )
+            std = small.tile([P, 1], F32, name="std")
+            nc.scalar.activation(
+                out=std[:], in_=sq_sum[:], func=ACT.Sqrt, scale=1.0 / EMBED, bias=eps_col[:]
+            )
+            rstd = small.tile([P, 1], F32, name="rstd")
+            nc.vector.reciprocal(out=rstd[:], in_=std[:])
+            h_bf = work.tile([P, EMBED], BF16, name="h_bf")
+            nc.vector.scalar_tensor_tensor(
+                out=h_bf[:],
+                in0=gained[:],
+                scalar=rstd[:],
+                in1=spread[:, AT_LN_B : AT_LN_B + EMBED],
+                op0=ALU.mult,
+                op1=ALU.add,
+            )
+            h_tiles[bt] = h_bf
+
+        def quantise_embedding(bt):
+            h_bf = h_tiles[bt]
+            h_flip = acc_psum.tile([P, PACK, P], BF16, name="h_flip", tag="acc%d" % bt)
+            for t in range(PACK):
+                nc.tensor.transpose(h_flip[:, t, :], h_bf[:, t * P : (t + 1) * P], ident_bf[:])
+            h_grouped = work.tile([P, P, PACK], BF16, name="h_grouped", align_bytes=64)
+            nc.scalar.copy(out=h_grouped[:], in_=h_flip[:].rearrange("e t b -> e b t"))
+            h_codes = work.tile([P, P], U32, name="h_codes", align_bytes=64)
+            h_scales = work.tile([P, P], U8, name="h_scales", align_bytes=64)
+            nc.vector.quantize_mx(
+                out=h_codes[:].bitcast(FP8X4),
+                scales=h_scales[:],
+                in_=h_grouped[:].rearrange("e b t -> e (b t)"),
+            )
+            h_code_tiles[bt] = (h_codes, h_scales)
+
+        def capsules(bt):
+            h_codes, h_scales = h_code_tiles[bt]
+            prim = acc_psum.tile([P, CAP_OUT], F32, name="prim", tag="acc%d" % bt)
+            nc.tensor.matmul_mx(
+                out=prim[:],
+                lhsT=h_codes[:].bitcast(FP8X4),
+                lhsT_scale=h_scales[:],
+                rhs=pcw_codes[:].bitcast(FP8X4),
+                rhs_scale=pcw_scales[:],
+                start=True,
+                stop=True,
+            )
+            by_capsule = [P, CAPSULES, CAP_DIM]
+            x = work.tile(by_capsule, F32, name="x")
+            nc.vector.tensor_tensor(
+                out=x[:].rearrange("b n p -> b (n p)"),
+                in0=prim[:],
+                in1=spread[:, AT_PC_B : AT_PC_B + CAP_OUT],
+                op=ALU.add,
+            )
+            x_sum = small.tile([P, CAPSULES], F32, name="x_sum")
+            nc.vector.reduce_sum(out=x_sum[:], in_=x[:], axis=AX.X)
+            centred = work.tile(by_capsule, F32, name="centred")
+            nc.vector.scalar_tensor_tensor(
+                out=centred[:],
+                in0=x_sum[:].unsqueeze(2).to_broadcast(by_capsule),
+                scalar=-1.0 / CAP_DIM,
+                in1=x[:],
+                op0=ALU.mult,
+                op1=ALU.add,
+            )
+            cap_squares = work.tile(by_capsule, F32, name="cap_squares")
+            nc.scalar.activation(out=cap_squares[:], in_=centred[:], func=ACT.Square)
+            cap_gained = work.tile(by_capsule, F32, name="cap_gained")
+            nc.vector.tensor_tensor(
+                out=cap_gained[:].rearrange("b n p -> b (n p)"),
+                in0=centred[:].rearrange("b n p -> b (n p)"),
+                in1=spread[:, AT_PC_G : AT_PC_G + CAP_OUT],
+                op=ALU.mult,
+            )
+            cap_sq_sum = small.tile([P, CAPSULES], F32, name="cap_sq_sum")
+            nc.vector.reduce_sum(out=cap_sq_sum[:], in_=cap_squares[:], axis=AX.X)
+            cap_std = small.tile([P, CAPSULES], F32, name="cap_std")
+            nc.scalar.activation(
+                out=cap_std[:], in_=cap_sq_sum[:], func=ACT.Sqrt, scale=1.0 / CAP_DIM, bias=eps_col[:]
+            )
+            cap_rstd = small.tile([P, CAPSULES], F32, name="cap_rstd")
+            nc.vector.reciprocal(out=cap_rstd[:], in_=cap_std[:])
+            normed = work.tile(by_capsule, F32, name="normed")
+            nc.vector.tensor_tensor(
+                out=normed[:],
+                in0=cap_gained[:],
+                in1=cap_rstd[:].unsqueeze(2).to_broadcast(by_capsule),
+                op=ALU.mult,
+            )
+            result = work.tile([P, CAP_OUT], F32, name="result")
+            nc.vector.tensor_tensor(
+                out=result[:],
+                in0=normed[:].rearrange("b n p -> b (n p)"),
+                in1=spread[:, AT_PC_BETA : AT_PC_BETA + CAP_OUT],
+                op=ALU.add,
+            )
+            nc.sync.dma_start(
+                out=out[bt * P : (bt + 1) * P].rearrange("b n p -> b (n p)"), in_=result[:]
+            )
+
+        first_closing = n_rounds - B_TILES
+        for r in range(n_rounds + 2):
+            if r + LOADS_AHEAD < n_rounds:
+                load_h1(r + LOADS_AHEAD)
+                if next_quarter < PASSES // QUARTER_PASSES:
+                    load_w2_quarter(next_quarter)
+                    next_quarter += 1
+            if r + 2 < n_rounds:
+                sort_words(r + 2)
+            if r + 1 < n_rounds:
+                transpose_round(r + 1)
+                quantise_round(r + 1)
+            if 0 <= r - first_closing - 2 < B_TILES:
+                capsules(r - first_closing - 2)
+            if r < n_rounds:
+                multiply_round(r)
+            if 0 <= r - first_closing - 1 < B_TILES:
+                quantise_embedding(r - first_closing - 1)
+            if 0 <= r - first_closing < B_TILES:
+                norm_embedding(r - first_closing)

@@ -33,7 +33,9 @@ PASS_WORDS = K_PASS // 2
 BANK_PASSES = 2
 QUARTER_PASSES = 2
 PLANES = 4
-LOADS_AHEAD = 4
+LOADS_AHEAD = 3
+SHARED_CHUNKS = 2
+VECTOR_SORTS = 6
 
 FLOPS = 2 * BATCH * HIDDEN * EMBED + 2 * BATCH * EMBED * CAP_OUT
 
@@ -50,8 +52,10 @@ def tile_hotpatchcapsmodel_pa_k_kernel(
     tc, h1, W2_words, W2_scales, b2, ln_g, ln_b, pc_W, pc_b, pc_g, pc_beta, out
 ):
     nc = tc.nc
-    rounds = [(chunk, bt) for chunk in range(CHUNKS) for bt in range(B_TILES)]
+    rounds = [(chunk, bt) for chunk in range(SHARED_CHUNKS) for bt in range(B_TILES)]
+    rounds += [(chunk, bt) for bt in range(B_TILES) for chunk in range(SHARED_CHUNKS, CHUNKS)]
     n_rounds = len(rounds)
+    closes = {r: bt for r, (chunk, bt) in enumerate(rounds) if chunk == CHUNKS - 1}
 
     with ExitStack() as ctx:
         const = ctx.enter_context(tc.tile_pool(name="const", bufs=1))
@@ -126,10 +130,11 @@ def tile_hotpatchcapsmodel_pa_k_kernel(
         def sort_words(r):
             words = raw_tiles[r][:].bitcast(F32)
             sorted_words = stage.tile([P, CHUNK_PASSES, 2, P], F32, name="sorted_words")
+            by_parity = words.rearrange("b (g j u) -> b g u j", g=CHUNK_PASSES, u=2)
             nc.vector.tensor_copy(
-                out=sorted_words[:],
-                in_=words.rearrange("b (g j u) -> b g u j", g=CHUNK_PASSES, u=2),
+                out=sorted_words[:, :VECTOR_SORTS], in_=by_parity[:, :VECTOR_SORTS]
             )
+            nc.scalar.copy(out=sorted_words[:, VECTOR_SORTS:], in_=by_parity[:, VECTOR_SORTS:])
             sorted_tiles[r] = sorted_words
 
         def transpose_round(r):
@@ -182,16 +187,26 @@ def tile_hotpatchcapsmodel_pa_k_kernel(
                     stop=(g == PASSES - 1),
                 )
 
+        chunks_loaded = set()
+
+        def load_for(r):
+            if r + 1 < n_rounds:
+                load_h1(r + 1)
+            chunk = rounds[r][0]
+            if chunk not in chunks_loaded:
+                chunks_loaded.add(chunk)
+                per_chunk = CHUNK_PASSES // QUARTER_PASSES
+                for q in range(chunk * per_chunk, (chunk + 1) * per_chunk):
+                    load_w2_quarter(q)
+
         load_h1(0)
         load_h1(1)
         load_w2_scales()
+        chunks_loaded.add(0)
         for q in range(CHUNK_PASSES // QUARTER_PASSES):
             load_w2_quarter(q)
-        next_quarter = CHUNK_PASSES // QUARTER_PASSES
-        for r in range(2, LOADS_AHEAD):
-            load_h1(r)
-            load_w2_quarter(next_quarter)
-            next_quarter += 1
+        for r in range(1, LOADS_AHEAD):
+            load_for(r)
 
         sort_words(0)
         sort_words(1)
@@ -352,23 +367,19 @@ def tile_hotpatchcapsmodel_pa_k_kernel(
                 out=out[bt * P : (bt + 1) * P].rearrange("b n p -> b (n p)"), in_=result[:]
             )
 
-        first_closing = n_rounds - B_TILES
         for r in range(n_rounds + 2):
             if r + LOADS_AHEAD < n_rounds:
-                load_h1(r + LOADS_AHEAD)
-                if next_quarter < PASSES // QUARTER_PASSES:
-                    load_w2_quarter(next_quarter)
-                    next_quarter += 1
+                load_for(r + LOADS_AHEAD)
             if r + 2 < n_rounds:
                 sort_words(r + 2)
             if r + 1 < n_rounds:
                 transpose_round(r + 1)
                 quantise_round(r + 1)
-            if 0 <= r - first_closing - 2 < B_TILES:
-                capsules(r - first_closing - 2)
+            if r - 2 in closes:
+                capsules(closes[r - 2])
             if r < n_rounds:
                 multiply_round(r)
-            if 0 <= r - first_closing - 1 < B_TILES:
-                quantise_embedding(r - first_closing - 1)
-            if 0 <= r - first_closing < B_TILES:
-                norm_embedding(r - first_closing)
+            if r - 1 in closes:
+                quantise_embedding(closes[r - 1])
+            if r in closes:
+                norm_embedding(closes[r])

@@ -34,7 +34,7 @@ BANK_PASSES = 2
 QUARTER_PASSES = 2
 PLANES = 4
 LOADS_AHEAD = 3
-SHARED_CHUNKS = 2
+SHARED_CHUNKS = 4
 VECTOR_SORTS = 6
 
 FLOPS = 2 * BATCH * HIDDEN * EMBED + 2 * BATCH * EMBED * CAP_OUT
@@ -52,10 +52,23 @@ def tile_hotpatchcapsmodel_pa_k_kernel(
     tc, h1, W2_words, W2_scales, b2, ln_g, ln_b, pc_W, pc_b, pc_g, pc_beta, out
 ):
     nc = tc.nc
-    rounds = [(chunk, bt) for chunk in range(SHARED_CHUNKS) for bt in range(B_TILES)]
-    rounds += [(chunk, bt) for bt in range(B_TILES) for chunk in range(SHARED_CHUNKS, CHUNKS)]
+    per_chunk = CHUNK_PASSES // QUARTER_PASSES
+    rounds = [
+        [(bt, QUARTER_PASSES * q + i) for bt in range(B_TILES) for i in range(QUARTER_PASSES)]
+        for q in range(per_chunk)
+    ]
+    rounds += [
+        [(bt, chunk * CHUNK_PASSES + i) for i in range(CHUNK_PASSES)]
+        for chunk in range(1, SHARED_CHUNKS)
+        for bt in range(B_TILES)
+    ]
+    rounds += [
+        [(bt, chunk * CHUNK_PASSES + i) for i in range(CHUNK_PASSES)]
+        for bt in range(B_TILES)
+        for chunk in range(SHARED_CHUNKS, CHUNKS)
+    ]
     n_rounds = len(rounds)
-    closes = {r: bt for r, (chunk, bt) in enumerate(rounds) if chunk == CHUNKS - 1}
+    closes = {r: slots[-1][0] for r, slots in enumerate(rounds) if slots[-1][1] == PASSES - 1}
 
     with ExitStack() as ctx:
         const = ctx.enter_context(tc.tile_pool(name="const", bufs=1))
@@ -101,12 +114,19 @@ def tile_hotpatchcapsmodel_pa_k_kernel(
         acc = {}
 
         def load_h1(r):
-            chunk, bt = rounds[r]
+            slots = rounds[r]
             raw = raw_pool.tile([P, CHUNK_K], BF16, name="raw")
-            nc.sync.dma_start(
-                out=raw[:],
-                in_=h1[bt * P : (bt + 1) * P, chunk * CHUNK_K : (chunk + 1) * CHUNK_K],
-            )
+            first = 0
+            while first < CHUNK_PASSES:
+                bt, g = slots[first]
+                n = 1
+                while first + n < CHUNK_PASSES and slots[first + n] == (bt, g + n):
+                    n += 1
+                nc.sync.dma_start(
+                    out=raw[:, first * K_PASS : (first + n) * K_PASS],
+                    in_=h1[bt * P : (bt + 1) * P, g * K_PASS : (g + n) * K_PASS],
+                )
+                first += n
             raw_tiles[r] = raw
 
         def load_w2_scales():
@@ -131,9 +151,11 @@ def tile_hotpatchcapsmodel_pa_k_kernel(
             words = raw_tiles[r][:].bitcast(F32)
             sorted_words = stage.tile([P, CHUNK_PASSES, 2, P], F32, name="sorted_words")
             by_parity = words.rearrange("b (g j u) -> b g u j", g=CHUNK_PASSES, u=2)
-            nc.vector.tensor_copy(
-                out=sorted_words[:, :VECTOR_SORTS], in_=by_parity[:, :VECTOR_SORTS]
-            )
+            step = QUARTER_PASSES if r == 0 else VECTOR_SORTS
+            for lo in range(0, VECTOR_SORTS, step):
+                nc.vector.tensor_copy(
+                    out=sorted_words[:, lo : lo + step], in_=by_parity[:, lo : lo + step]
+                )
             nc.scalar.copy(out=sorted_words[:, VECTOR_SORTS:], in_=by_parity[:, VECTOR_SORTS:])
             sorted_tiles[r] = sorted_words
 
@@ -170,12 +192,11 @@ def tile_hotpatchcapsmodel_pa_k_kernel(
             code_tiles[r] = (codes, scales)
 
         def multiply_round(r):
-            chunk, bt = rounds[r]
             codes, scales = code_tiles[r]
-            if chunk == 0:
-                acc[bt] = acc_psum.tile([P, EMBED], F32, name="acc%d" % bt)
             for i in range(CHUNK_PASSES):
-                g = chunk * CHUNK_PASSES + i
+                bt, g = rounds[r][i]
+                if g == 0:
+                    acc[bt] = acc_psum.tile([P, EMBED], F32, name="acc%d" % bt)
                 cols = slice(i * P, (i + 1) * P)
                 nc.tensor.matmul_mx(
                     out=acc[bt][:],
@@ -187,25 +208,20 @@ def tile_hotpatchcapsmodel_pa_k_kernel(
                     stop=(g == PASSES - 1),
                 )
 
-        chunks_loaded = set()
+        quarters_loaded = set()
 
         def load_for(r):
             if r + 1 < n_rounds:
                 load_h1(r + 1)
-            chunk = rounds[r][0]
-            if chunk not in chunks_loaded:
-                chunks_loaded.add(chunk)
-                per_chunk = CHUNK_PASSES // QUARTER_PASSES
-                for q in range(chunk * per_chunk, (chunk + 1) * per_chunk):
+            for bt, g in rounds[r]:
+                q = g // QUARTER_PASSES
+                if q not in quarters_loaded:
+                    quarters_loaded.add(q)
                     load_w2_quarter(q)
 
         load_h1(0)
-        load_h1(1)
         load_w2_scales()
-        chunks_loaded.add(0)
-        for q in range(CHUNK_PASSES // QUARTER_PASSES):
-            load_w2_quarter(q)
-        for r in range(1, LOADS_AHEAD):
+        for r in range(LOADS_AHEAD):
             load_for(r)
 
         sort_words(0)

@@ -35,6 +35,7 @@ QUARTER_PASSES = 2
 PLANES = 4
 LOADS_AHEAD = 3
 SHARED_CHUNKS = 4
+FINE_CHUNKS = 2
 VECTOR_SORTS = 6
 
 FLOPS = 2 * BATCH * HIDDEN * EMBED + 2 * BATCH * EMBED * CAP_OUT
@@ -55,11 +56,11 @@ def tile_hotpatchcapsmodel_pa_k_kernel(
     per_chunk = CHUNK_PASSES // QUARTER_PASSES
     rounds = [
         [(bt, QUARTER_PASSES * q + i) for bt in range(B_TILES) for i in range(QUARTER_PASSES)]
-        for q in range(per_chunk)
+        for q in range(FINE_CHUNKS * per_chunk)
     ]
     rounds += [
         [(bt, chunk * CHUNK_PASSES + i) for i in range(CHUNK_PASSES)]
-        for chunk in range(1, SHARED_CHUNKS)
+        for chunk in range(FINE_CHUNKS, SHARED_CHUNKS)
         for bt in range(B_TILES)
     ]
     rounds += [
@@ -117,6 +118,15 @@ def tile_hotpatchcapsmodel_pa_k_kernel(
             slots = rounds[r]
             raw = raw_pool.tile([P, CHUNK_K], BF16, name="raw")
             first = 0
+            if 0 < r < FINE_CHUNKS * per_chunk:
+                g = slots[0][1]
+                nc.sync.dma_start(
+                    out=raw[:].rearrange("p (t k) -> p t k", t=B_TILES),
+                    in_=h1.rearrange("(t p) k -> p t k", p=P)[
+                        :, :, g * K_PASS : (g + QUARTER_PASSES) * K_PASS
+                    ],
+                )
+                first = CHUNK_PASSES
             while first < CHUNK_PASSES:
                 bt, g = slots[first]
                 n = 1

@@ -83,7 +83,7 @@ def tile_hotpatchcapsmodel_pa_k_kernel(
 
         vec_row = const.tile([P, ROW_WIDTH], BF16)
         nc.vector.memset(vec_row[:], 0.0)
-        w2_planes = const.tile([P, PASSES // PLANES, EMBED], U8, align_bytes=64)
+        w2_planes = const.tile([P, PASSES // PLANES, EMBED], U8, align_bytes=256)
         nc.vector.memset(w2_planes[:].bitcast(I32), 0)
         ones = const.tile([P, P], BF16)
         nc.vector.memset(ones[:], 1.0)
@@ -91,11 +91,11 @@ def tile_hotpatchcapsmodel_pa_k_kernel(
         nc.vector.memset(eps_col[:], EPS)
         table_warm = const.tile([P, 1], F32)
         nc.scalar.activation(out=table_warm[:], in_=eps_col[:], func=ACT.Sqrt)
-        ident_f32 = const.tile([P, P], F32)
+        ident_f32 = const.tile([P, P], F32, align_bytes=256)
         make_identity(nc, ident_f32[:])
         ident_bf = const.tile([P, P], BF16)
         make_identity(nc, ident_bf[:])
-        w2_codes = const.tile([P, PASSES, EMBED], U32, align_bytes=64)
+        w2_codes = const.tile([P, PASSES, EMBED], U32, align_bytes=256)
 
         pcw_raw = const.tile([P, P * CAP_DIM], BF16)
         nc.scalar.dma_start(out=pcw_raw[:], in_=pc_W.rearrange("n (a e) p -> (n a) (e p)", e=P))
@@ -116,7 +116,7 @@ def tile_hotpatchcapsmodel_pa_k_kernel(
 
         def load_h1(r):
             slots = rounds[r]
-            raw = raw_pool.tile([P, CHUNK_K], BF16, name="raw")
+            raw = raw_pool.tile([P, CHUNK_K], BF16, name="raw", align_bytes=256)
             first = 0
             if 0 < r < FINE_CHUNKS * per_chunk:
                 g = slots[0][1]
@@ -159,7 +159,7 @@ def tile_hotpatchcapsmodel_pa_k_kernel(
 
         def sort_words(r):
             words = raw_tiles[r][:].bitcast(F32)
-            sorted_words = stage.tile([P, CHUNK_PASSES, 2, P], F32, name="sorted_words")
+            sorted_words = stage.tile([P, CHUNK_PASSES, 2, P], F32, name="sorted_words", align_bytes=256)
             by_parity = words.rearrange("b (g j u) -> b g u j", g=CHUNK_PASSES, u=2)
             step = QUARTER_PASSES if r == 0 else VECTOR_SORTS
             for lo in range(0, VECTOR_SORTS, step):
@@ -171,7 +171,7 @@ def tile_hotpatchcapsmodel_pa_k_kernel(
 
         def transpose_round(r):
             sorted_words = sorted_tiles[r]
-            grouped = stage.tile([P, CHUNK_K], BF16, name="grouped", align_bytes=64)
+            grouped = stage.tile([P, CHUNK_K], BF16, name="grouped", align_bytes=256)
             grouped_words = grouped[:].bitcast(F32).rearrange(
                 "p (g b u) -> p g b u", g=CHUNK_PASSES, u=2
             )
@@ -190,8 +190,8 @@ def tile_hotpatchcapsmodel_pa_k_kernel(
 
         def quantise_round(r):
             grouped = grouped_tiles[r]
-            codes = codes_pool.tile([P, CHUNK_PASSES * P], U32, name="codes", align_bytes=64)
-            scales = codes_pool.tile([P, CHUNK_PASSES * P], U8, name="scales", align_bytes=64)
+            codes = codes_pool.tile([P, CHUNK_PASSES * P], U32, name="codes", align_bytes=256)
+            scales = codes_pool.tile([P, CHUNK_PASSES * P], U8, name="scales", align_bytes=256)
             half = CHUNK_PASSES * P // 2
             for lo in (0, half):
                 nc.vector.quantize_mx(

@@ -26,87 +26,56 @@ EPS = 1e-5
 
 B_TILES = BATCH // P
 PASSES = HIDDEN // K_PASS
-CHUNK_PASSES = 8
-CHUNKS = PASSES // CHUNK_PASSES
-CHUNK_K = CHUNK_PASSES * K_PASS
-PASS_WORDS = K_PASS // 2
+UNIT = 4
+UNIT_K = UNIT * K_PASS
+GROUPS = PASSES // UNIT
+SHARED = 5
 BANK_PASSES = 2
-QUARTER_PASSES = 2
-PLANES = 4
-LOADS_AHEAD = 3
-SHARED_CHUNKS = 4
-FINE_CHUNKS = 2
-VECTOR_SORTS = 6
+PLANES = UNIT
+LOAD_AHEAD = 9
 
 FLOPS = 2 * BATCH * HIDDEN * EMBED + 2 * BATCH * EMBED * CAP_OUT
 
+ROW_GAIN = 0
+ROW_SHIFT = 4
+ROW_B2 = 8
+ROW_PC = 12
 AT_B2 = 0
-AT_LN_G = EMBED
-AT_LN_B = 2 * EMBED
-AT_PC_B = 3 * EMBED
-AT_PC_G = 3 * EMBED + CAP_OUT
-AT_PC_BETA = 3 * EMBED + 2 * CAP_OUT
-ROW_WIDTH = 3 * EMBED + 3 * CAP_OUT
+AT_PC_B = EMBED
+AT_PC_G = EMBED + CAP_OUT
+AT_PC_BETA = EMBED + 2 * CAP_OUT
+SPREAD = EMBED + 3 * CAP_OUT
 
 
 def tile_hotpatchcapsmodel_pa_k_kernel(
     tc, h1, W2_words, W2_scales, b2, ln_g, ln_b, pc_W, pc_b, pc_g, pc_beta, out
 ):
     nc = tc.nc
-    per_chunk = CHUNK_PASSES // QUARTER_PASSES
-    rounds = [
-        [(bt, QUARTER_PASSES * q + i) for bt in range(B_TILES) for i in range(QUARTER_PASSES)]
-        for q in range(FINE_CHUNKS * per_chunk)
-    ]
-    rounds += [
-        [(bt, chunk * CHUNK_PASSES + i) for i in range(CHUNK_PASSES)]
-        for chunk in range(FINE_CHUNKS, SHARED_CHUNKS)
-        for bt in range(B_TILES)
-    ]
-    rounds += [
-        [(bt, chunk * CHUNK_PASSES + i) for i in range(CHUNK_PASSES)]
-        for bt in range(B_TILES)
-        for chunk in range(SHARED_CHUNKS, CHUNKS)
-    ]
-    n_rounds = len(rounds)
-    closes = {r: slots[-1][0] for r, slots in enumerate(rounds) if slots[-1][1] == PASSES - 1}
+    units = [(bt, sb) for sb in range(SHARED) for bt in range(B_TILES)]
+    for tiles in ((0,), (1,), (2, 3)):
+        units += [(bt, sb) for sb in range(SHARED, GROUPS) for bt in tiles]
+    n_units = len(units)
 
     with ExitStack() as ctx:
+        ctx.enter_context(tc.manual_schedule())
         const = ctx.enter_context(tc.tile_pool(name="const", bufs=1))
-        raw_pool = ctx.enter_context(tc.tile_pool(name="raw", bufs=6))
-        stage = ctx.enter_context(tc.tile_pool(name="stage", bufs=2))
-        codes_pool = ctx.enter_context(tc.tile_pool(name="codes", bufs=3))
+        raw_pool = ctx.enter_context(tc.tile_pool(name="raw", bufs=10))
+        stage = ctx.enter_context(tc.tile_pool(name="stage", bufs=3))
+        codes_pool = ctx.enter_context(tc.tile_pool(name="codes", bufs=4))
         work = ctx.enter_context(tc.tile_pool(name="work", bufs=2))
         small = ctx.enter_context(tc.tile_pool(name="small", bufs=2))
         flip_psum = ctx.enter_context(tc.psum_pool(name="flip", bufs=4))
         acc_psum = ctx.enter_context(tc.psum_pool(name="acc", bufs=1))
 
-        vec_row = const.tile([P, ROW_WIDTH], BF16)
-        nc.vector.memset(vec_row[:], 0.0)
-        w2_planes = const.tile([P, PASSES // PLANES, EMBED], U8, align_bytes=256)
-        nc.vector.memset(w2_planes[:].bitcast(I32), 0)
-        ones = const.tile([P, P], BF16)
-        nc.vector.memset(ones[:], 1.0)
-        eps_col = const.tile([P, 1], F32)
-        nc.vector.memset(eps_col[:], EPS)
-        table_warm = const.tile([P, 1], F32)
-        nc.scalar.activation(out=table_warm[:], in_=eps_col[:], func=ACT.Sqrt)
-        ident_f32 = const.tile([P, P], F32, align_bytes=256)
-        make_identity(nc, ident_f32[:])
-        ident_bf = const.tile([P, P], BF16)
-        make_identity(nc, ident_bf[:])
         w2_codes = const.tile([P, PASSES, EMBED], U32, align_bytes=256)
-
+        first_planes = const.tile([P, UNIT, EMBED], U8, align_bytes=256)
+        w2_planes = const.tile([P, GROUPS - 1, EMBED], U8, align_bytes=256)
+        vec_rows = const.tile([P, P], BF16)
         pcw_raw = const.tile([P, P * CAP_DIM], BF16)
-        nc.scalar.dma_start(out=pcw_raw[:], in_=pc_W.rearrange("n (a e) p -> (n a) (e p)", e=P))
-        for vec, at in ((b2, AT_B2), (ln_g, AT_LN_G), (ln_b, AT_LN_B)):
-            nc.scalar.dma_start(
-                out=vec_row[0:1, at : at + EMBED], in_=vec.rearrange("(o e) -> o e", o=1)
-            )
-        for vec, at in ((pc_b, AT_PC_B), (pc_g, AT_PC_G), (pc_beta, AT_PC_BETA)):
-            nc.scalar.dma_start(
-                out=vec_row[0:1, at : at + CAP_OUT], in_=vec.rearrange("(o n) p -> o (n p)", o=1)
-            )
+        eps_col = const.tile([P, 1], F32)
+        table_warm = const.tile([P, 1], F32)
+        ident_f32 = const.tile([P, P], F32, align_bytes=256)
+        ident_bf = const.tile([P, P], BF16)
 
         raw_tiles = {}
         sorted_tiles = {}
@@ -114,68 +83,70 @@ def tile_hotpatchcapsmodel_pa_k_kernel(
         code_tiles = {}
         acc = {}
 
-        def load_h1(r):
-            slots = rounds[r]
-            raw = raw_pool.tile([P, CHUNK_K], BF16, name="raw", align_bytes=256)
-            first = 0
-            if 0 < r < FINE_CHUNKS * per_chunk:
-                g = slots[0][1]
+        def load_h1(n, pieces=1):
+            bt, sb = units[n]
+            raw = raw_pool.tile([P, UNIT_K], BF16, name="raw", align_bytes=256)
+            width = UNIT_K // pieces
+            for i in range(pieces):
                 nc.sync.dma_start(
-                    out=raw[:].rearrange("p (t k) -> p t k", t=B_TILES),
-                    in_=h1.rearrange("(t p) k -> p t k", p=P)[
-                        :, :, g * K_PASS : (g + QUARTER_PASSES) * K_PASS
-                    ],
+                    out=raw[:, i * width : (i + 1) * width],
+                    in_=h1[bt * P : (bt + 1) * P, sb * UNIT_K + i * width : sb * UNIT_K + (i + 1) * width],
                 )
-                first = CHUNK_PASSES
-            while first < CHUNK_PASSES:
-                bt, g = slots[first]
-                n = 1
-                while first + n < CHUNK_PASSES and slots[first + n] == (bt, g + n):
-                    n += 1
-                nc.sync.dma_start(
-                    out=raw[:, first * K_PASS : (first + n) * K_PASS],
-                    in_=h1[bt * P : (bt + 1) * P, g * K_PASS : (g + n) * K_PASS],
-                )
-                first += n
-            raw_tiles[r] = raw
+            raw_tiles[n] = raw
 
-        def load_w2_scales():
-            for quadrant in range(4):
-                for plane in range(PLANES):
-                    first = 32 * quadrant + 4 * plane
-                    nc.sync.dma_start(
-                        out=w2_planes[first : first + 4, :, :].bitcast(I32),
-                        in_=W2_scales[plane:PASSES:PLANES, 4 * quadrant : 4 * quadrant + 4, :]
-                        .rearrange("s r n -> r s n")
-                        .bitcast(I32),
-                    )
-
-        def load_w2_quarter(q):
-            passes = slice(q * QUARTER_PASSES, (q + 1) * QUARTER_PASSES)
+        def load_w2(first, count):
+            passes = slice(first, first + count)
             nc.sync.dma_start(
                 out=w2_codes[:, passes, :].bitcast(I32),
                 in_=W2_words[passes].rearrange("g p n t -> p g (n t)").bitcast(I32),
             )
 
-        def sort_words(r):
-            words = raw_tiles[r][:].bitcast(F32)
-            sorted_words = stage.tile([P, CHUNK_PASSES, 2, P], F32, name="sorted_words", align_bytes=256)
-            by_parity = words.rearrange("b (g j u) -> b g u j", g=CHUNK_PASSES, u=2)
-            step = QUARTER_PASSES if r == 0 else VECTOR_SORTS
-            for lo in range(0, VECTOR_SORTS, step):
+        def load_first_scales():
+            for quadrant in range(4):
+                nc.sync.dma_start(
+                    out=first_planes[32 * quadrant : 32 * quadrant + 4, :, :].bitcast(I32),
+                    in_=W2_scales[0:UNIT, 4 * quadrant : 4 * quadrant + 4, :]
+                    .rearrange("s r n -> r s n")
+                    .bitcast(I32),
+                )
+
+        def load_scales(quadrant):
+            if True:
+                for plane in range(PLANES):
+                    first = 32 * quadrant + 4 * plane
+                    nc.sync.dma_start(
+                        out=w2_planes[first : first + 4, :, :].bitcast(I32),
+                        in_=W2_scales[UNIT + plane : PASSES : PLANES, 4 * quadrant : 4 * quadrant + 4, :]
+                        .rearrange("s r n -> r s n")
+                        .bitcast(I32),
+                    )
+
+        def load_small():
+            nc.sync.dma_start(out=pcw_raw[:], in_=pc_W.rearrange("n (a e) p -> (n a) (e p)", e=P))
+            for vec, row in ((b2, ROW_B2), (ln_g, ROW_GAIN), (ln_b, ROW_SHIFT)):
+                nc.sync.dma_start(out=vec_rows[row : row + 4, :], in_=vec.rearrange("(r e) -> r e", e=P))
+            for i, vec in enumerate((pc_b, pc_g, pc_beta)):
+                nc.sync.dma_start(
+                    out=vec_rows[ROW_PC + 2 * i : ROW_PC + 2 * i + 2, :],
+                    in_=vec.rearrange("(r n) p -> r (n p)", r=2),
+                )
+
+        def sort(n, pieces=1):
+            words = raw_tiles[n][:].bitcast(F32)
+            by_parity = words.rearrange("b (g j u) -> b g u j", g=UNIT, u=2)
+            sorted_words = stage.tile([P, UNIT, 2, P], F32, name="sorted_words", align_bytes=256)
+            step = UNIT // pieces
+            for lo in range(0, UNIT, step):
                 nc.vector.tensor_copy(
                     out=sorted_words[:, lo : lo + step], in_=by_parity[:, lo : lo + step]
                 )
-            nc.scalar.copy(out=sorted_words[:, VECTOR_SORTS:], in_=by_parity[:, VECTOR_SORTS:])
-            sorted_tiles[r] = sorted_words
+            sorted_tiles[n] = sorted_words
 
-        def transpose_round(r):
-            sorted_words = sorted_tiles[r]
-            grouped = stage.tile([P, CHUNK_K], BF16, name="grouped", align_bytes=256)
-            grouped_words = grouped[:].bitcast(F32).rearrange(
-                "p (g b u) -> p g b u", g=CHUNK_PASSES, u=2
-            )
-            for first in range(0, CHUNK_PASSES, BANK_PASSES):
+        def flip(n):
+            sorted_words = sorted_tiles[n]
+            grouped = stage.tile([P, UNIT_K], BF16, name="grouped", align_bytes=256)
+            grouped_words = grouped[:].bitcast(F32).rearrange("p (g b u) -> p g b u", g=UNIT, u=2)
+            for first in range(0, UNIT, BANK_PASSES):
                 bank = flip_psum.tile([P, BANK_PASSES, 2, P], F32, name="bank", tag="flip")
                 for i in range(BANK_PASSES):
                     for u in range(2):
@@ -186,206 +157,250 @@ def tile_hotpatchcapsmodel_pa_k_kernel(
                     out=grouped_words[:, first : first + BANK_PASSES],
                     in_=bank[:].rearrange("p g u b -> p g b u"),
                 )
-            grouped_tiles[r] = grouped
+            grouped_tiles[n] = grouped
 
-        def quantise_round(r):
-            grouped = grouped_tiles[r]
-            codes = codes_pool.tile([P, CHUNK_PASSES * P], U32, name="codes", align_bytes=256)
-            scales = codes_pool.tile([P, CHUNK_PASSES * P], U8, name="scales", align_bytes=256)
-            half = CHUNK_PASSES * P // 2
-            for lo in (0, half):
-                nc.vector.quantize_mx(
-                    out=codes[:, lo : lo + half].bitcast(FP8X4),
-                    scales=scales[:, lo : lo + half],
-                    in_=grouped[:, PACK * lo : PACK * (lo + half)],
-                )
-            code_tiles[r] = (codes, scales)
+        def quantise(n):
+            codes = codes_pool.tile([P, UNIT * P], U32, name="codes", align_bytes=256)
+            scales = codes_pool.tile([P, UNIT * P], U8, name="scales", align_bytes=256)
+            nc.vector.quantize_mx(
+                out=codes[:].bitcast(FP8X4), scales=scales[:], in_=grouped_tiles[n][:]
+            )
+            code_tiles[n] = (codes, scales)
 
-        def multiply_round(r):
-            codes, scales = code_tiles[r]
-            for i in range(CHUNK_PASSES):
-                bt, g = rounds[r][i]
-                if g == 0:
-                    acc[bt] = acc_psum.tile([P, EMBED], F32, name="acc%d" % bt)
+        def multiply(n):
+            bt, sb = units[n]
+            codes, scales = code_tiles[n]
+            if sb == 0:
+                acc[bt] = acc_psum.tile([P, EMBED], F32, name="acc%d" % bt)
+            for i in range(UNIT):
+                g = sb * UNIT + i
                 cols = slice(i * P, (i + 1) * P)
+                if sb == 0:
+                    plane = first_planes[:, i, :]
+                else:
+                    plane = w2_planes[4 * i : P, sb - 1, :]
                 nc.tensor.matmul_mx(
                     out=acc[bt][:],
                     lhsT=codes[:, cols].bitcast(FP8X4),
                     lhsT_scale=scales[:, cols],
                     rhs=w2_codes[:, g, :].bitcast(FP8X4),
-                    rhs_scale=w2_planes[4 * (g % PLANES) : P, g // PLANES, :],
+                    rhs_scale=plane,
                     start=(g == 0),
                     stop=(g == PASSES - 1),
                 )
 
-        quarters_loaded = set()
-
-        def load_for(r):
-            if r + 1 < n_rounds:
-                load_h1(r + 1)
-            for bt, g in rounds[r]:
-                q = g // QUARTER_PASSES
-                if q not in quarters_loaded:
-                    quarters_loaded.add(q)
-                    load_w2_quarter(q)
-
-        load_h1(0)
-        load_w2_scales()
-        for r in range(LOADS_AHEAD):
-            load_for(r)
-
-        sort_words(0)
-        sort_words(1)
-        transpose_round(0)
-        quantise_round(0)
-
-        spread = const.tile([P, ROW_WIDTH], F32)
-        for lo in range(0, ROW_WIDTH, EMBED):
-            width = min(EMBED, ROW_WIDTH - lo)
-            rep = flip_psum.tile([P, width], F32, name="rep", tag="flip")
-            nc.tensor.matmul(
-                out=rep[:], lhsT=ones[:], rhs=vec_row[:, lo : lo + width], start=True, stop=True
-            )
-            nc.scalar.copy(out=spread[:, lo : lo + width], in_=rep[:])
-
+        spread = const.tile([P, SPREAD], BF16)
+        gain_shift = const.tile([P, 8], F32)
         pcw_sorted = const.tile([P, CAP_DIM, P], BF16)
-        nc.vector.tensor_copy(
-            out=pcw_sorted[:], in_=pcw_raw[:].rearrange("q (e p) -> q p e", p=CAP_DIM)
-        )
-        pcw_flip = flip_psum.tile([P, CAP_DIM, P], BF16, name="pcw_flip", tag="flip")
-        for p in range(CAP_DIM):
-            nc.tensor.transpose(pcw_flip[:, p, :], pcw_sorted[:, p, :], ident_bf[:])
         pcw_grouped = const.tile([P, CAPSULES, CAP_DIM, PACK], BF16, align_bytes=64)
-        nc.vector.tensor_copy(
-            out=pcw_grouped[:], in_=pcw_flip[:].rearrange("e p (n a) -> e n p a", a=PACK)
-        )
         pcw_codes = const.tile([P, CAP_OUT], U32, align_bytes=64)
         pcw_scales = const.tile([P, CAP_OUT], U8, align_bytes=64)
-        nc.vector.quantize_mx(
-            out=pcw_codes[:].bitcast(FP8X4),
-            scales=pcw_scales[:],
-            in_=pcw_grouped[:].rearrange("e n p a -> e (n p a)"),
-        )
 
-        h_tiles = {}
-        h_code_tiles = {}
+        def spread_rows(first, count, at):
+            rep = flip_psum.tile([P, count * P], BF16, name="rep", tag="flip")
+            for r in range(count):
+                nc.tensor.matmul(
+                    out=rep[:, r * P : (r + 1) * P],
+                    lhsT=ident_bf[:, first + r : first + r + 1].to_broadcast([P, P]),
+                    rhs=vec_rows[:],
+                    start=True,
+                    stop=True,
+                )
+            nc.scalar.copy(out=spread[:, at : at + count * P], in_=rep[:])
 
-        def norm_embedding(bt):
-            biased = work.tile([P, EMBED], F32, name="biased")
+        def flip_gains():
+            rep = flip_psum.tile([P, P], BF16, name="rep", tag="flip")
+            nc.tensor.transpose(rep[:], vec_rows[:], ident_bf[:])
+            nc.scalar.copy(out=gain_shift[:], in_=rep[:, ROW_GAIN : ROW_SHIFT + 4])
+
+        def sort_pcw():
+            nc.vector.tensor_copy(
+                out=pcw_sorted[:], in_=pcw_raw[:].rearrange("q (e p) -> q p e", p=CAP_DIM)
+            )
+
+        def flip_pcw():
+            pcw_flip = flip_psum.tile([P, CAP_DIM, P], BF16, name="pcw_flip", tag="flip")
+            for p in range(CAP_DIM):
+                nc.tensor.transpose(pcw_flip[:, p, :], pcw_sorted[:, p, :], ident_bf[:])
+            nc.scalar.copy(
+                out=pcw_grouped[:], in_=pcw_flip[:].rearrange("e p (n a) -> e n p a", a=PACK)
+            )
+
+        def quantise_pcw():
+            nc.vector.quantize_mx(
+                out=pcw_codes[:].bitcast(FP8X4),
+                scales=pcw_scales[:],
+                in_=pcw_grouped[:].rearrange("e n p a -> e (n p a)"),
+            )
+
+        t = {}
+
+        def new(bt, pool, shape, dtype, what, **kw):
+            t[what, bt] = pool.tile(shape, dtype, name=what, **kw)
+            return t[what, bt]
+
+        def add_bias(bt):
+            biased = new(bt, work, [P, EMBED], F32, "biased")
             nc.vector.tensor_tensor(
                 out=biased[:], in0=acc[bt][:], in1=spread[:, AT_B2 : AT_B2 + EMBED], op=ALU.add
             )
-            z = work.tile([P, EMBED], F32, name="z")
-            z_sum = small.tile([P, 1], F32, name="z_sum")
-            nc.scalar.activation(out=z[:], in_=biased[:], func=ACT.Relu, accum_out=z_sum[:])
-            neg_mean = small.tile([P, 1], F32, name="neg_mean")
-            nc.vector.tensor_scalar_mul(out=neg_mean[:], in0=z_sum[:], scalar1=-1.0 / EMBED)
-            squares = work.tile([P, EMBED], F32, name="squares")
-            sq_sum = small.tile([P, 1], F32, name="sq_sum")
+
+        def rectify(bt):
+            z = new(bt, work, [P, EMBED], F32, "z")
+            z_sum = new(bt, small, [P, 1], F32, "z_sum")
+            nc.scalar.activation(out=z[:], in_=t["biased", bt][:], func=ACT.Relu, accum_out=z_sum[:])
+
+        def negate_mean(bt):
+            neg_mean = new(bt, small, [P, 1], F32, "neg_mean")
+            nc.vector.tensor_scalar_mul(out=neg_mean[:], in0=t["z_sum", bt][:], scalar1=-1.0 / EMBED)
+
+        def square(bt):
+            squares = new(bt, work, [P, EMBED], F32, "squares")
+            sq_sum = new(bt, small, [P, 1], F32, "sq_sum")
             nc.scalar.activation(
-                out=squares[:], in_=z[:], func=ACT.Square, bias=neg_mean[:], accum_out=sq_sum[:]
+                out=squares[:],
+                in_=t["z", bt][:],
+                func=ACT.Square,
+                bias=t["neg_mean", bt][:],
+                accum_out=sq_sum[:],
             )
-            gained = work.tile([P, EMBED], F32, name="gained")
-            nc.vector.scalar_tensor_tensor(
-                out=gained[:],
-                in0=z[:],
-                scalar=neg_mean[:],
-                in1=spread[:, AT_LN_G : AT_LN_G + EMBED],
+
+        def root(bt):
+            std = new(bt, small, [P, 1], F32, "std")
+            nc.scalar.activation(
+                out=std[:], in_=t["sq_sum", bt][:], func=ACT.Sqrt, scale=1.0 / EMBED, bias=eps_col[:]
+            )
+
+        def norm(bt):
+            rstd = new(bt, small, [P, 1], F32, "rstd")
+            nc.vector.reciprocal(out=rstd[:], in_=t["std", bt][:])
+            normed = new(bt, work, [P, EMBED], F32, "normed_z")
+            nc.vector.tensor_scalar(
+                out=normed[:],
+                in0=t["z", bt][:],
+                scalar1=t["neg_mean", bt][:],
+                scalar2=rstd[:],
                 op0=ALU.add,
                 op1=ALU.mult,
             )
-            std = small.tile([P, 1], F32, name="std")
-            nc.scalar.activation(
-                out=std[:], in_=sq_sum[:], func=ACT.Sqrt, scale=1.0 / EMBED, bias=eps_col[:]
-            )
-            rstd = small.tile([P, 1], F32, name="rstd")
-            nc.vector.reciprocal(out=rstd[:], in_=std[:])
-            h_bf = work.tile([P, EMBED], BF16, name="h_bf")
-            nc.vector.scalar_tensor_tensor(
-                out=h_bf[:],
-                in0=gained[:],
-                scalar=rstd[:],
-                in1=spread[:, AT_LN_B : AT_LN_B + EMBED],
-                op0=ALU.mult,
-                op1=ALU.add,
-            )
-            h_tiles[bt] = h_bf
 
-        def quantise_embedding(bt):
-            h_bf = h_tiles[bt]
-            h_flip = acc_psum.tile([P, PACK, P], BF16, name="h_flip", tag="acc%d" % bt)
-            for t in range(PACK):
-                nc.tensor.transpose(h_flip[:, t, :], h_bf[:, t * P : (t + 1) * P], ident_bf[:])
-            h_grouped = work.tile([P, P, PACK], BF16, name="h_grouped", align_bytes=64)
-            nc.scalar.copy(out=h_grouped[:], in_=h_flip[:].rearrange("e t b -> e b t"))
-            h_codes = work.tile([P, P], U32, name="h_codes", align_bytes=64)
-            h_scales = work.tile([P, P], U8, name="h_scales", align_bytes=64)
+        def flip_norm(bt):
+            h_flip = new(bt, acc_psum, [P, PACK, P], F32, "h_flip", tag="acc%d" % bt)
+            for i in range(PACK):
+                nc.tensor.transpose(
+                    h_flip[:, i, :], t["normed_z", bt][:, i * P : (i + 1) * P], ident_f32[:]
+                )
+
+        def gain_and_shift(bt):
+            h = new(bt, work, [P, PACK, P], BF16, "h")
+            for i in range(PACK):
+                nc.scalar.activation(
+                    out=h[:, i, :],
+                    in_=t["h_flip", bt][:, i, :],
+                    func=ACT.Identity,
+                    scale=gain_shift[:, ROW_GAIN + i : ROW_GAIN + i + 1],
+                    bias=gain_shift[:, ROW_SHIFT + i : ROW_SHIFT + i + 1],
+                )
+
+        def group_h(bt):
+            h_grouped = new(bt, work, [P, P, PACK], BF16, "h_grouped", align_bytes=64)
+            nc.vector.tensor_copy(out=h_grouped[:], in_=t["h", bt][:].rearrange("e i b -> e b i"))
+
+        def quantise_h(bt):
+            h_codes = new(bt, work, [P, P], U32, "h_codes", align_bytes=64)
+            h_scales = new(bt, work, [P, P], U8, "h_scales", align_bytes=64)
             nc.vector.quantize_mx(
                 out=h_codes[:].bitcast(FP8X4),
                 scales=h_scales[:],
-                in_=h_grouped[:].rearrange("e b t -> e (b t)"),
+                in_=t["h_grouped", bt][:].rearrange("e b i -> e (b i)"),
             )
-            h_code_tiles[bt] = (h_codes, h_scales)
 
-        def capsules(bt):
-            h_codes, h_scales = h_code_tiles[bt]
-            prim = acc_psum.tile([P, CAP_OUT], F32, name="prim", tag="acc%d" % bt)
+        def multiply_h(bt):
+            prim = new(bt, acc_psum, [P, CAP_OUT], F32, "prim", tag="acc%d" % bt)
             nc.tensor.matmul_mx(
                 out=prim[:],
-                lhsT=h_codes[:].bitcast(FP8X4),
-                lhsT_scale=h_scales[:],
+                lhsT=t["h_codes", bt][:].bitcast(FP8X4),
+                lhsT_scale=t["h_scales", bt][:],
                 rhs=pcw_codes[:].bitcast(FP8X4),
                 rhs_scale=pcw_scales[:],
                 start=True,
                 stop=True,
             )
-            by_capsule = [P, CAPSULES, CAP_DIM]
-            x = work.tile(by_capsule, F32, name="x")
+
+        by_capsule = [P, CAPSULES, CAP_DIM]
+
+        def flat(ap):
+            return ap.rearrange("b n p -> b (n p)")
+
+        def cap_bias(bt):
+            x = new(bt, work, by_capsule, F32, "x")
             nc.vector.tensor_tensor(
-                out=x[:].rearrange("b n p -> b (n p)"),
-                in0=prim[:],
+                out=flat(x[:]),
+                in0=t["prim", bt][:],
                 in1=spread[:, AT_PC_B : AT_PC_B + CAP_OUT],
                 op=ALU.add,
             )
-            x_sum = small.tile([P, CAPSULES], F32, name="x_sum")
-            nc.vector.reduce_sum(out=x_sum[:], in_=x[:], axis=AX.X)
-            centred = work.tile(by_capsule, F32, name="centred")
+
+        def cap_sum(bt):
+            x_sum = new(bt, small, [P, CAPSULES], F32, "x_sum")
+            nc.vector.reduce_sum(out=x_sum[:], in_=t["x", bt][:], axis=AX.X)
+
+        def cap_centre(bt):
+            centred = new(bt, work, by_capsule, F32, "centred")
             nc.vector.scalar_tensor_tensor(
                 out=centred[:],
-                in0=x_sum[:].unsqueeze(2).to_broadcast(by_capsule),
+                in0=t["x_sum", bt][:].unsqueeze(2).to_broadcast(by_capsule),
                 scalar=-1.0 / CAP_DIM,
-                in1=x[:],
+                in1=t["x", bt][:],
                 op0=ALU.mult,
                 op1=ALU.add,
             )
-            cap_squares = work.tile(by_capsule, F32, name="cap_squares")
-            nc.scalar.activation(out=cap_squares[:], in_=centred[:], func=ACT.Square)
-            cap_gained = work.tile(by_capsule, F32, name="cap_gained")
+
+        def cap_square(bt):
+            cap_squares = new(bt, work, by_capsule, F32, "cap_squares")
+            nc.scalar.activation(out=cap_squares[:], in_=t["centred", bt][:], func=ACT.Square)
+
+        def cap_gain(bt):
+            gained = new(bt, work, by_capsule, F32, "cap_gained")
             nc.vector.tensor_tensor(
-                out=cap_gained[:].rearrange("b n p -> b (n p)"),
-                in0=centred[:].rearrange("b n p -> b (n p)"),
+                out=flat(gained[:]),
+                in0=flat(t["centred", bt][:]),
                 in1=spread[:, AT_PC_G : AT_PC_G + CAP_OUT],
                 op=ALU.mult,
             )
-            cap_sq_sum = small.tile([P, CAPSULES], F32, name="cap_sq_sum")
-            nc.vector.reduce_sum(out=cap_sq_sum[:], in_=cap_squares[:], axis=AX.X)
-            cap_std = small.tile([P, CAPSULES], F32, name="cap_std")
+
+        def cap_square_sum(bt):
+            cap_sq_sum = new(bt, small, [P, CAPSULES], F32, "cap_sq_sum")
+            nc.vector.reduce_sum(out=cap_sq_sum[:], in_=t["cap_squares", bt][:], axis=AX.X)
+
+        def cap_root(bt):
+            cap_std = new(bt, small, [P, CAPSULES], F32, "cap_std")
             nc.scalar.activation(
-                out=cap_std[:], in_=cap_sq_sum[:], func=ACT.Sqrt, scale=1.0 / CAP_DIM, bias=eps_col[:]
+                out=cap_std[:],
+                in_=t["cap_sq_sum", bt][:],
+                func=ACT.Sqrt,
+                scale=1.0 / CAP_DIM,
+                bias=eps_col[:],
             )
-            cap_rstd = small.tile([P, CAPSULES], F32, name="cap_rstd")
-            nc.vector.reciprocal(out=cap_rstd[:], in_=cap_std[:])
-            normed = work.tile(by_capsule, F32, name="normed")
+
+        def cap_invert(bt):
+            cap_rstd = new(bt, small, [P, CAPSULES], F32, "cap_rstd")
+            nc.vector.reciprocal(out=cap_rstd[:], in_=t["cap_std", bt][:])
+
+        def cap_norm(bt):
+            normed = new(bt, work, by_capsule, F32, "normed")
             nc.vector.tensor_tensor(
                 out=normed[:],
-                in0=cap_gained[:],
-                in1=cap_rstd[:].unsqueeze(2).to_broadcast(by_capsule),
+                in0=t["cap_gained", bt][:],
+                in1=t["cap_rstd", bt][:].unsqueeze(2).to_broadcast(by_capsule),
                 op=ALU.mult,
             )
-            result = work.tile([P, CAP_OUT], F32, name="result")
+
+        def cap_shift(bt):
+            result = new(bt, work, [P, CAP_OUT], F32, "result")
             nc.vector.tensor_tensor(
                 out=result[:],
-                in0=normed[:].rearrange("b n p -> b (n p)"),
+                in0=flat(t["normed", bt][:]),
                 in1=spread[:, AT_PC_BETA : AT_PC_BETA + CAP_OUT],
                 op=ALU.add,
             )
@@ -393,19 +408,89 @@ def tile_hotpatchcapsmodel_pa_k_kernel(
                 out=out[bt * P : (bt + 1) * P].rearrange("b n p -> b (n p)"), in_=result[:]
             )
 
-        for r in range(n_rounds + 2):
-            if r + LOADS_AHEAD < n_rounds:
-                load_for(r + LOADS_AHEAD)
-            if r + 2 < n_rounds:
-                sort_words(r + 2)
-            if r + 1 < n_rounds:
-                transpose_round(r + 1)
-                quantise_round(r + 1)
-            if r - 2 in closes:
-                capsules(closes[r - 2])
-            if r < n_rounds:
-                multiply_round(r)
-            if r - 1 in closes:
-                quantise_embedding(closes[r - 1])
-            if r in closes:
-                norm_embedding(closes[r])
+        ending = [
+            ((add_bias,), (rectify,)),
+            ((negate_mean,), (square,)),
+            ((), (root,)),
+            ((norm,), ()),
+            ((flip_norm,), (gain_and_shift,)),
+            ((group_h,), ()),
+            ((quantise_h,), ()),
+            ((multiply_h,), ()),
+            ((cap_bias, cap_sum), ()),
+            ((cap_centre,), (cap_square,)),
+            ((cap_gain, cap_square_sum), (cap_root,)),
+            ((cap_invert, cap_norm), ()),
+            ((cap_shift,), ()),
+        ]
+
+        nc.vector.memset(first_planes[:].bitcast(I32), 0)
+        nc.vector.memset(eps_col[:], EPS)
+        nc.vector.memset(w2_planes[:].bitcast(I32), 0)
+        nc.vector.memset(vec_rows[:].bitcast(I32), 0)
+        nc.scalar.activation(out=table_warm[:], in_=eps_col[:], func=ACT.Sqrt)
+        make_identity(nc, ident_f32[:])
+        make_identity(nc, ident_bf[:])
+
+        load_h1(0, pieces=2)
+        load_first_scales()
+        load_w2(0, 2)
+        load_h1(1)
+        load_w2(2, 2)
+        load_scales(0)
+        load_h1(2)
+        load_scales(1)
+        load_h1(3)
+        load_scales(2)
+        load_w2(4, 2)
+        load_scales(3)
+        load_h1(4)
+        load_w2(6, 2)
+        load_small()
+        next_w2 = 2 * UNIT
+        next_h1 = 5
+
+        sort(0, pieces=2)
+        flip(0)
+        sort(1)
+        quantise(0)
+        flip(1)
+        sort(2)
+
+        prepare = {2: (flip_gains,), 3: (sort_pcw,), 4: (flip_pcw,), 5: (quantise_pcw,)}
+        prepare[6] = (lambda: spread_rows(ROW_B2, 8, AT_B2),)
+        prepare[7] = (lambda: spread_rows(ROW_PC + 4, 2, AT_PC_BETA),)
+        active = []
+
+        def advance(part):
+            for bt, steps in active:
+                if steps:
+                    for f in steps[0][part]:
+                        f(bt)
+                    if part == 1:
+                        steps.pop(0)
+
+        for n in range(n_units):
+            while next_h1 < min(n + LOAD_AHEAD, n_units):
+                bt, sb = units[next_h1]
+                if sb * UNIT >= next_w2:
+                    load_w2(next_w2, UNIT)
+                    next_w2 += UNIT
+                load_h1(next_h1)
+                next_h1 += 1
+            multiply(n)
+            if n + 1 < n_units:
+                quantise(n + 1)
+            if n + 2 < n_units:
+                flip(n + 2)
+            if n + 3 < n_units:
+                sort(n + 3)
+            for f in prepare.get(n, ()):
+                f()
+            advance(0)
+            advance(1)
+            if units[n][1] == GROUPS - 1:
+                active.append((units[n][0], list(ending)))
+        while any(steps for bt, steps in active):
+            advance(0)
+            advance(1)

@@ -31,7 +31,6 @@ UNIT_K = UNIT * K_PASS
 GROUPS = PASSES // UNIT
 SHARED = 5
 BANK_PASSES = 2
-PLANES = UNIT
 LOAD_AHEAD = 9
 
 FLOPS = 2 * BATCH * HIDDEN * EMBED + 2 * BATCH * EMBED * CAP_OUT
@@ -52,7 +51,7 @@ def tile_hotpatchcapsmodel_pa_k_kernel(
 ):
     nc = tc.nc
     units = [(bt, sb) for sb in range(SHARED) for bt in range(B_TILES)]
-    for tiles in ((0,), (1,), (2, 3)):
+    for tiles in ((0,), (1,), (2,), (3,)):
         units += [(bt, sb) for sb in range(SHARED, GROUPS) for bt in tiles]
     n_units = len(units)
 
@@ -68,8 +67,7 @@ def tile_hotpatchcapsmodel_pa_k_kernel(
         acc_psum = ctx.enter_context(tc.psum_pool(name="acc", bufs=1))
 
         w2_codes = const.tile([P, PASSES, EMBED], U32, align_bytes=256)
-        first_planes = const.tile([P, UNIT, EMBED], U8, align_bytes=256)
-        w2_planes = const.tile([P, GROUPS - 1, EMBED], U8, align_bytes=256)
+        w2_planes = const.tile([P, GROUPS, EMBED], U8, align_bytes=256)
         vec_rows = const.tile([P, P], BF16)
         pcw_raw = const.tile([P, P * CAP_DIM], BF16)
         eps_col = const.tile([P, 1], F32)
@@ -101,32 +99,19 @@ def tile_hotpatchcapsmodel_pa_k_kernel(
                 in_=W2_words[passes].rearrange("g p n t -> p g (n t)").bitcast(I32),
             )
 
-        def load_first_scales():
+        def load_scales(sb):
             for quadrant in range(4):
                 nc.sync.dma_start(
-                    out=first_planes[32 * quadrant : 32 * quadrant + 4, :, :].bitcast(I32),
-                    in_=W2_scales[0:UNIT, 4 * quadrant : 4 * quadrant + 4, :]
-                    .rearrange("s r n -> r s n")
-                    .bitcast(I32),
+                    out=w2_planes[32 * quadrant : 32 * quadrant + 4 * UNIT, sb, :].bitcast(I32),
+                    in_=W2_scales[sb * UNIT : (sb + 1) * UNIT, 4 * quadrant : 4 * quadrant + 4, :].bitcast(I32),
                 )
 
-        def load_scales(quadrant):
-            if True:
-                for plane in range(PLANES):
-                    first = 32 * quadrant + 4 * plane
-                    nc.sync.dma_start(
-                        out=w2_planes[first : first + 4, :, :].bitcast(I32),
-                        in_=W2_scales[UNIT + plane : PASSES : PLANES, 4 * quadrant : 4 * quadrant + 4, :]
-                        .rearrange("s r n -> r s n")
-                        .bitcast(I32),
-                    )
-
         def load_small():
-            nc.sync.dma_start(out=pcw_raw[:], in_=pc_W.rearrange("n (a e) p -> (n a) (e p)", e=P))
+            nc.gpsimd.dma_start(out=pcw_raw[:], in_=pc_W.rearrange("n (a e) p -> (n a) (e p)", e=P))
             for vec, row in ((b2, ROW_B2), (ln_g, ROW_GAIN), (ln_b, ROW_SHIFT)):
-                nc.sync.dma_start(out=vec_rows[row : row + 4, :], in_=vec.rearrange("(r e) -> r e", e=P))
+                nc.gpsimd.dma_start(out=vec_rows[row : row + 4, :], in_=vec.rearrange("(r e) -> r e", e=P))
             for i, vec in enumerate((pc_b, pc_g, pc_beta)):
-                nc.sync.dma_start(
+                nc.gpsimd.dma_start(
                     out=vec_rows[ROW_PC + 2 * i : ROW_PC + 2 * i + 2, :],
                     in_=vec.rearrange("(r n) p -> r (n p)", r=2),
                 )
@@ -159,12 +144,16 @@ def tile_hotpatchcapsmodel_pa_k_kernel(
                 )
             grouped_tiles[n] = grouped
 
-        def quantise(n):
+        def quantise(n, pieces=1):
             codes = codes_pool.tile([P, UNIT * P], U32, name="codes", align_bytes=256)
             scales = codes_pool.tile([P, UNIT * P], U8, name="scales", align_bytes=256)
-            nc.vector.quantize_mx(
-                out=codes[:].bitcast(FP8X4), scales=scales[:], in_=grouped_tiles[n][:]
-            )
+            width = UNIT * P // pieces
+            for lo in range(0, UNIT * P, width):
+                nc.vector.quantize_mx(
+                    out=codes[:, lo : lo + width].bitcast(FP8X4),
+                    scales=scales[:, lo : lo + width],
+                    in_=grouped_tiles[n][:, PACK * lo : PACK * (lo + width)],
+                )
             code_tiles[n] = (codes, scales)
 
         def multiply(n):
@@ -175,22 +164,20 @@ def tile_hotpatchcapsmodel_pa_k_kernel(
             for i in range(UNIT):
                 g = sb * UNIT + i
                 cols = slice(i * P, (i + 1) * P)
-                if sb == 0:
-                    plane = first_planes[:, i, :]
-                else:
-                    plane = w2_planes[4 * i : P, sb - 1, :]
                 nc.tensor.matmul_mx(
                     out=acc[bt][:],
                     lhsT=codes[:, cols].bitcast(FP8X4),
                     lhsT_scale=scales[:, cols],
                     rhs=w2_codes[:, g, :].bitcast(FP8X4),
-                    rhs_scale=plane,
+                    rhs_scale=w2_planes[4 * i : P, sb, :],
                     start=(g == 0),
                     stop=(g == PASSES - 1),
                 )
 
         spread = const.tile([P, SPREAD], BF16)
         gain_shift = const.tile([P, 8], F32)
+        bias_sum = const.tile([P, CAPSULES], F32)
+        centred_bias = const.tile([P, CAP_OUT], F32)
         pcw_sorted = const.tile([P, CAP_DIM, P], BF16)
         pcw_grouped = const.tile([P, CAPSULES, CAP_DIM, PACK], BF16, align_bytes=64)
         pcw_codes = const.tile([P, CAP_OUT], U32, align_bytes=64)
@@ -207,6 +194,18 @@ def tile_hotpatchcapsmodel_pa_k_kernel(
                     stop=True,
                 )
             nc.scalar.copy(out=spread[:, at : at + count * P], in_=rep[:])
+
+        def centre_bias():
+            bias = spread[:, AT_PC_B : AT_PC_B + CAP_OUT].rearrange("b (n p) -> b n p", p=CAP_DIM)
+            nc.vector.reduce_sum(out=bias_sum[:], in_=bias, axis=AX.X)
+            nc.vector.scalar_tensor_tensor(
+                out=centred_bias[:].rearrange("b (n p) -> b n p", p=CAP_DIM),
+                in0=bias_sum[:].unsqueeze(2).to_broadcast([P, CAPSULES, CAP_DIM]),
+                scalar=-1.0 / CAP_DIM,
+                in1=bias,
+                op0=ALU.mult,
+                op1=ALU.add,
+            )
 
         def flip_gains():
             rep = flip_psum.tile([P, P], BF16, name="rep", tag="flip")
@@ -261,25 +260,28 @@ def tile_hotpatchcapsmodel_pa_k_kernel(
                 out=squares[:],
                 in_=t["z", bt][:],
                 func=ACT.Square,
-                bias=t["neg_mean", bt][:],
+                scale=-float(EMBED),
+                bias=t["z_sum", bt][:],
                 accum_out=sq_sum[:],
             )
 
         def root(bt):
-            std = new(bt, small, [P, 1], F32, "std")
+            rstd = new(bt, small, [P, 1], F32, "rstd")
             nc.scalar.activation(
-                out=std[:], in_=t["sq_sum", bt][:], func=ACT.Sqrt, scale=1.0 / EMBED, bias=eps_col[:]
+                out=rstd[:],
+                in_=t["sq_sum", bt][:],
+                func=ACT.Abs_reciprocal_sqrt,
+                scale=1.0 / EMBED**3,
+                bias=eps_col[:],
             )
 
         def norm(bt):
-            rstd = new(bt, small, [P, 1], F32, "rstd")
-            nc.vector.reciprocal(out=rstd[:], in_=t["std", bt][:])
             normed = new(bt, work, [P, EMBED], F32, "normed_z")
             nc.vector.tensor_scalar(
                 out=normed[:],
                 in0=t["z", bt][:],
                 scalar1=t["neg_mean", bt][:],
-                scalar2=rstd[:],
+                scalar2=t["rstd", bt][:],
                 op0=ALU.add,
                 op1=ALU.mult,
             )
@@ -293,14 +295,27 @@ def tile_hotpatchcapsmodel_pa_k_kernel(
 
         def gain_and_shift(bt):
             h = new(bt, work, [P, PACK, P], BF16, "h")
+            by_vector = PACK // 2 if bt == B_TILES - 1 else 0
             for i in range(PACK):
-                nc.scalar.activation(
-                    out=h[:, i, :],
-                    in_=t["h_flip", bt][:, i, :],
-                    func=ACT.Identity,
-                    scale=gain_shift[:, ROW_GAIN + i : ROW_GAIN + i + 1],
-                    bias=gain_shift[:, ROW_SHIFT + i : ROW_SHIFT + i + 1],
-                )
+                gain = gain_shift[:, ROW_GAIN + i : ROW_GAIN + i + 1]
+                shift = gain_shift[:, ROW_SHIFT + i : ROW_SHIFT + i + 1]
+                if i >= PACK - by_vector:
+                    nc.vector.tensor_scalar(
+                        out=h[:, i, :],
+                        in0=t["h_flip", bt][:, i, :],
+                        scalar1=gain,
+                        scalar2=shift,
+                        op0=ALU.mult,
+                        op1=ALU.add,
+                    )
+                else:
+                    nc.scalar.activation(
+                        out=h[:, i, :],
+                        in_=t["h_flip", bt][:, i, :],
+                        func=ACT.Identity,
+                        scale=gain,
+                        bias=shift,
+                    )
 
         def group_h(bt):
             h_grouped = new(bt, work, [P, P, PACK], BF16, "h_grouped", align_bytes=64)
@@ -332,153 +347,176 @@ def tile_hotpatchcapsmodel_pa_k_kernel(
         def flat(ap):
             return ap.rearrange("b n p -> b (n p)")
 
+        def parts(bt):
+            half = CAPSULES // 2
+            return (slice(0, half), slice(half, CAPSULES)) if bt == B_TILES - 1 else (slice(0, CAPSULES),)
+
+        def columns(part):
+            return slice(part.start * CAP_DIM, part.stop * CAP_DIM)
+
         def cap_bias(bt):
             x = new(bt, work, by_capsule, F32, "x")
-            nc.vector.tensor_tensor(
-                out=flat(x[:]),
-                in0=t["prim", bt][:],
-                in1=spread[:, AT_PC_B : AT_PC_B + CAP_OUT],
-                op=ALU.add,
-            )
+            for part in parts(bt):
+                nc.vector.tensor_tensor(
+                    out=flat(x[:, part]),
+                    in0=t["prim", bt][:, columns(part)],
+                    in1=centred_bias[:, columns(part)],
+                    op=ALU.add,
+                )
 
         def cap_sum(bt):
             x_sum = new(bt, small, [P, CAPSULES], F32, "x_sum")
-            nc.vector.reduce_sum(out=x_sum[:], in_=t["x", bt][:], axis=AX.X)
+            for part in parts(bt):
+                nc.vector.reduce_sum(
+                    out=x_sum[:, part],
+                    in_=t["prim", bt][:, columns(part)].rearrange("b (n p) -> b n p", p=CAP_DIM),
+                    axis=AX.X,
+                )
 
         def cap_centre(bt):
             centred = new(bt, work, by_capsule, F32, "centred")
-            nc.vector.scalar_tensor_tensor(
-                out=centred[:],
-                in0=t["x_sum", bt][:].unsqueeze(2).to_broadcast(by_capsule),
-                scalar=-1.0 / CAP_DIM,
-                in1=t["x", bt][:],
-                op0=ALU.mult,
-                op1=ALU.add,
-            )
+            for part in parts(bt):
+                shape = [P, part.stop - part.start, CAP_DIM]
+                nc.vector.scalar_tensor_tensor(
+                    out=centred[:, part],
+                    in0=t["x_sum", bt][:, part].unsqueeze(2).to_broadcast(shape),
+                    scalar=-1.0 / CAP_DIM,
+                    in1=t["x", bt][:, part],
+                    op0=ALU.mult,
+                    op1=ALU.add,
+                )
 
         def cap_square(bt):
             cap_squares = new(bt, work, by_capsule, F32, "cap_squares")
-            nc.scalar.activation(out=cap_squares[:], in_=t["centred", bt][:], func=ACT.Square)
+            for part in parts(bt):
+                nc.scalar.activation(
+                    out=cap_squares[:, part], in_=t["centred", bt][:, part], func=ACT.Square
+                )
 
         def cap_gain(bt):
             gained = new(bt, work, by_capsule, F32, "cap_gained")
-            nc.vector.tensor_tensor(
-                out=flat(gained[:]),
-                in0=flat(t["centred", bt][:]),
-                in1=spread[:, AT_PC_G : AT_PC_G + CAP_OUT],
-                op=ALU.mult,
-            )
+            for part in parts(bt):
+                nc.vector.tensor_tensor(
+                    out=flat(gained[:, part]),
+                    in0=flat(t["centred", bt][:, part]),
+                    in1=spread[:, AT_PC_G : AT_PC_G + CAP_OUT][:, columns(part)],
+                    op=ALU.mult,
+                )
 
         def cap_square_sum(bt):
             cap_sq_sum = new(bt, small, [P, CAPSULES], F32, "cap_sq_sum")
-            nc.vector.reduce_sum(out=cap_sq_sum[:], in_=t["cap_squares", bt][:], axis=AX.X)
+            for part in parts(bt):
+                nc.vector.reduce_sum(
+                    out=cap_sq_sum[:, part], in_=t["cap_squares", bt][:, part], axis=AX.X
+                )
 
         def cap_root(bt):
-            cap_std = new(bt, small, [P, CAPSULES], F32, "cap_std")
-            nc.scalar.activation(
-                out=cap_std[:],
-                in_=t["cap_sq_sum", bt][:],
-                func=ACT.Sqrt,
-                scale=1.0 / CAP_DIM,
-                bias=eps_col[:],
-            )
-
-        def cap_invert(bt):
             cap_rstd = new(bt, small, [P, CAPSULES], F32, "cap_rstd")
-            nc.vector.reciprocal(out=cap_rstd[:], in_=t["cap_std", bt][:])
+            for part in parts(bt):
+                nc.scalar.activation(
+                    out=cap_rstd[:, part],
+                    in_=t["cap_sq_sum", bt][:, part],
+                    func=ACT.Abs_reciprocal_sqrt,
+                    scale=1.0 / CAP_DIM,
+                    bias=eps_col[:],
+                )
 
         def cap_norm(bt):
             normed = new(bt, work, by_capsule, F32, "normed")
-            nc.vector.tensor_tensor(
-                out=normed[:],
-                in0=t["cap_gained", bt][:],
-                in1=t["cap_rstd", bt][:].unsqueeze(2).to_broadcast(by_capsule),
-                op=ALU.mult,
-            )
+            for part in parts(bt):
+                shape = [P, part.stop - part.start, CAP_DIM]
+                nc.vector.tensor_tensor(
+                    out=normed[:, part],
+                    in0=t["cap_gained", bt][:, part],
+                    in1=t["cap_rstd", bt][:, part].unsqueeze(2).to_broadcast(shape),
+                    op=ALU.mult,
+                )
 
         def cap_shift(bt):
             result = new(bt, work, [P, CAP_OUT], F32, "result")
-            nc.vector.tensor_tensor(
-                out=result[:],
-                in0=flat(t["normed", bt][:]),
-                in1=spread[:, AT_PC_BETA : AT_PC_BETA + CAP_OUT],
-                op=ALU.add,
-            )
-            nc.sync.dma_start(
-                out=out[bt * P : (bt + 1) * P].rearrange("b n p -> b (n p)"), in_=result[:]
-            )
+            for part in parts(bt):
+                nc.vector.tensor_tensor(
+                    out=result[:, columns(part)],
+                    in0=flat(t["normed", bt][:, part]),
+                    in1=spread[:, AT_PC_BETA : AT_PC_BETA + CAP_OUT][:, columns(part)],
+                    op=ALU.add,
+                )
+            for part in parts(bt):
+                nc.sync.dma_start(
+                    out=out[bt * P : (bt + 1) * P, part].rearrange("b n p -> b (n p)"),
+                    in_=result[:, columns(part)],
+                )
 
         ending = [
             ((add_bias,), (rectify,)),
-            ((negate_mean,), (square,)),
-            ((), (root,)),
+            ((negate_mean,), (square, root)),
             ((norm,), ()),
             ((flip_norm,), (gain_and_shift,)),
-            ((group_h,), ()),
-            ((quantise_h,), ()),
+            ((group_h, quantise_h), ()),
             ((multiply_h,), ()),
-            ((cap_bias, cap_sum), ()),
-            ((cap_centre,), (cap_square,)),
+            ((cap_sum, cap_bias, cap_centre), (cap_square,)),
             ((cap_gain, cap_square_sum), (cap_root,)),
-            ((cap_invert, cap_norm), ()),
-            ((cap_shift,), ()),
+            ((cap_norm, cap_shift), ()),
         ]
 
-        nc.vector.memset(first_planes[:].bitcast(I32), 0)
+        nc.vector.memset(w2_planes[:, 0, :].bitcast(I32), 0)
         nc.vector.memset(eps_col[:], EPS)
-        nc.vector.memset(w2_planes[:].bitcast(I32), 0)
         nc.vector.memset(vec_rows[:].bitcast(I32), 0)
-        nc.scalar.activation(out=table_warm[:], in_=eps_col[:], func=ACT.Sqrt)
+        nc.vector.memset(w2_planes[:, 1:GROUPS, :].bitcast(I32), 0)
+        nc.scalar.activation(out=table_warm[:], in_=eps_col[:], func=ACT.Abs_reciprocal_sqrt)
         make_identity(nc, ident_f32[:])
         make_identity(nc, ident_bf[:])
 
         load_h1(0, pieces=2)
-        load_first_scales()
-        load_w2(0, 2)
-        load_h1(1)
-        load_w2(2, 2)
         load_scales(0)
+        load_w2(0, 2)
+        load_w2(2, 2)
+        load_h1(1)
         load_h1(2)
-        load_scales(1)
         load_h1(3)
-        load_scales(2)
-        load_w2(4, 2)
-        load_scales(3)
-        load_h1(4)
-        load_w2(6, 2)
         load_small()
-        next_w2 = 2 * UNIT
-        next_h1 = 5
+        next_w2 = UNIT
+        next_h1 = 4
 
         sort(0, pieces=2)
         flip(0)
+        quantise(0, pieces=2)
+        multiply(0)
         sort(1)
-        quantise(0)
         flip(1)
         sort(2)
 
-        prepare = {2: (flip_gains,), 3: (sort_pcw,), 4: (flip_pcw,), 5: (quantise_pcw,)}
-        prepare[6] = (lambda: spread_rows(ROW_B2, 8, AT_B2),)
-        prepare[7] = (lambda: spread_rows(ROW_PC + 4, 2, AT_PC_BETA),)
+        prepare = {1: (sort_pcw,), 2: (flip_pcw,), 3: (quantise_pcw,), 7: (flip_gains,)}
+        prepare[8] = (lambda: spread_rows(ROW_B2, 8, AT_B2),)
+        prepare[9] = (lambda: spread_rows(ROW_PC + 4, 2, AT_PC_BETA), centre_bias)
         active = []
 
         def advance(part):
+            now = [(bt, steps[0][part]) for bt, steps in reversed(active) if steps]
+            for i in range(max([len(fs) for bt, fs in now], default=0)):
+                for bt, fs in now:
+                    if i < len(fs):
+                        fs[i](bt)
+
+        def drop():
             for bt, steps in active:
                 if steps:
-                    for f in steps[0][part]:
-                        f(bt)
-                    if part == 1:
-                        steps.pop(0)
+                    steps.remove(steps[0])
 
-        for n in range(n_units):
-            while next_h1 < min(n + LOAD_AHEAD, n_units):
-                bt, sb = units[next_h1]
-                if sb * UNIT >= next_w2:
-                    load_w2(next_w2, UNIT)
-                    next_w2 += UNIT
-                load_h1(next_h1)
-                next_h1 += 1
-            multiply(n)
+        loaded = [next_h1, next_w2]
+
+        def step(n):
+            while loaded[0] < min(n + LOAD_AHEAD, n_units):
+                sb = units[loaded[0]][1]
+                load_h1(loaded[0])
+                loaded[0] += 1
+                if sb * UNIT >= loaded[1]:
+                    load_scales(sb)
+                    load_w2(loaded[1], UNIT // 2)
+                    load_w2(loaded[1] + UNIT // 2, UNIT // 2)
+                    loaded[1] += UNIT
+            if n > 0:
+                multiply(n)
             if n + 1 < n_units:
                 quantise(n + 1)
             if n + 2 < n_units:
@@ -487,10 +525,20 @@ def tile_hotpatchcapsmodel_pa_k_kernel(
                 sort(n + 3)
             for f in prepare.get(n, ()):
                 f()
-            advance(0)
-            advance(1)
+            if n < n_units - 1:
+                advance(0)
+                advance(1)
+                drop()
             if units[n][1] == GROUPS - 1:
                 active.append((units[n][0], list(ending)))
-        while any(steps for bt, steps in active):
-            advance(0)
-            advance(1)
+
+        for n in range(n_units):
+            step(n)
+        rest = []
+        for bt, steps in reversed(active):
+            rest.append([(f, bt) for vector_part, scalar_part in steps for f in vector_part + scalar_part])
+        while any(rest):
+            for fs in rest:
+                for f, bt in fs[:1]:
+                    f(bt)
+                    fs.remove((f, bt))

@@ -27,10 +27,9 @@ EPS = 1e-5
 B_TILES = BATCH // P
 PASSES = HIDDEN // K_PASS
 UNIT = 4
+HALF = 2
 UNIT_K = UNIT * K_PASS
 GROUPS = PASSES // UNIT
-SHARED = 5
-BANK_PASSES = 2
 LOAD_AHEAD = 9
 
 FLOPS = 2 * BATCH * HIDDEN * EMBED + 2 * BATCH * EMBED * CAP_OUT
@@ -50,17 +49,22 @@ def tile_hotpatchcapsmodel_pa_k_kernel(
     tc, h1, W2_words, W2_scales, b2, ln_g, ln_b, pc_W, pc_b, pc_g, pc_beta, out
 ):
     nc = tc.nc
-    units = [(bt, sb) for sb in range(SHARED) for bt in range(B_TILES)]
-    for tiles in ((0,), (1,), (2,), (3,)):
-        units += [(bt, sb) for sb in range(SHARED, GROUPS) for bt in tiles]
+    def alone(bt, sb):
+        return [(bt, sb * UNIT + i) for i in range(UNIT)]
+
+    def in_pairs(bt, pair):
+        return [(b, pair * HALF + i) for b in (bt, bt + 1) for i in range(HALF)]
+
+    units = [in_pairs(bt, pair) for pair in range(2) for bt in range(0, B_TILES, 2)]
+    units += [alone(bt, sb) for sb in range(2 // 2, 5) for bt in range(B_TILES)]
+    units += [alone(bt, sb) for bt, sb in ((0, 5), (1, 5), (0, 6), (1, 6), (0, 7), (1, 7), (2, 5), (2, 6), (2, 7), (3, 5), (3, 6), (3, 7))]
     n_units = len(units)
 
     with ExitStack() as ctx:
-        ctx.enter_context(tc.manual_schedule())
         const = ctx.enter_context(tc.tile_pool(name="const", bufs=1))
-        raw_pool = ctx.enter_context(tc.tile_pool(name="raw", bufs=10))
-        stage = ctx.enter_context(tc.tile_pool(name="stage", bufs=3))
-        codes_pool = ctx.enter_context(tc.tile_pool(name="codes", bufs=4))
+        raw_pool = ctx.enter_context(tc.tile_pool(name="raw", bufs=12))
+        stage = ctx.enter_context(tc.tile_pool(name="stage", bufs=4))
+        codes_pool = ctx.enter_context(tc.tile_pool(name="codes", bufs=6))
         work = ctx.enter_context(tc.tile_pool(name="work", bufs=2))
         small = ctx.enter_context(tc.tile_pool(name="small", bufs=2))
         flip_psum = ctx.enter_context(tc.psum_pool(name="flip", bufs=4))
@@ -81,19 +85,29 @@ def tile_hotpatchcapsmodel_pa_k_kernel(
         code_tiles = {}
         acc = {}
 
-        def load_h1(n, pieces=1):
-            bt, sb = units[n]
+        def load_h1(n, apart=False):
+            slots = units[n]
             raw = raw_pool.tile([P, UNIT_K], BF16, name="raw", align_bytes=256)
-            width = UNIT_K // pieces
-            for i in range(pieces):
+            bt, g = slots[0]
+            tiles = 1 + slots[-1][0] - bt
+            passes = UNIT // tiles
+            if tiles == 1 or not apart:
                 nc.sync.dma_start(
-                    out=raw[:, i * width : (i + 1) * width],
-                    in_=h1[bt * P : (bt + 1) * P, sb * UNIT_K + i * width : sb * UNIT_K + (i + 1) * width],
+                    out=raw[:].rearrange("p (t k) -> p t k", t=tiles),
+                    in_=h1.rearrange("(t p) k -> p t k", p=P)[
+                        :, bt : bt + tiles, g * K_PASS : (g + passes) * K_PASS
+                    ],
                 )
+            else:
+                for i in range(tiles):
+                    nc.sync.dma_start(
+                        out=raw[:, i * passes * K_PASS : (i + 1) * passes * K_PASS],
+                        in_=h1[(bt + i) * P : (bt + i + 1) * P, g * K_PASS : (g + passes) * K_PASS],
+                    )
             raw_tiles[n] = raw
 
-        def load_w2(first, count):
-            passes = slice(first, first + count)
+        def load_w2(pair):
+            passes = slice(HALF * pair, HALF * (pair + 1))
             nc.sync.dma_start(
                 out=w2_codes[:, passes, :].bitcast(I32),
                 in_=W2_words[passes].rearrange("g p n t -> p g (n t)").bitcast(I32),
@@ -127,49 +141,50 @@ def tile_hotpatchcapsmodel_pa_k_kernel(
                 )
             sorted_tiles[n] = sorted_words
 
-        def flip(n):
-            sorted_words = sorted_tiles[n]
-            grouped = stage.tile([P, UNIT_K], BF16, name="grouped", align_bytes=256)
-            grouped_words = grouped[:].bitcast(F32).rearrange("p (g b u) -> p g b u", g=UNIT, u=2)
-            for first in range(0, UNIT, BANK_PASSES):
-                bank = flip_psum.tile([P, BANK_PASSES, 2, P], F32, name="bank", tag="flip")
-                for i in range(BANK_PASSES):
-                    for u in range(2):
-                        nc.tensor.transpose(
-                            bank[:, i, u, :], sorted_words[:, first + i, u, :], ident_f32[:]
-                        )
-                nc.scalar.copy(
-                    out=grouped_words[:, first : first + BANK_PASSES],
-                    in_=bank[:].rearrange("p g u b -> p g b u"),
-                )
-            grouped_tiles[n] = grouped
+        def flip(x):
+            n, half = divmod(x, 2)
+            if half == 0:
+                grouped_tiles[n] = stage.tile([P, UNIT_K], BF16, name="grouped", align_bytes=256)
+            grouped_words = grouped_tiles[n][:].bitcast(F32).rearrange("p (g b u) -> p g b u", g=UNIT, u=2)
+            bank = flip_psum.tile([P, HALF, 2, P], F32, name="bank", tag="flip")
+            for i in range(HALF):
+                for u in range(2):
+                    nc.tensor.transpose(
+                        bank[:, i, u, :], sorted_tiles[n][:, HALF * half + i, u, :], ident_f32[:]
+                    )
+            nc.scalar.copy(
+                out=grouped_words[:, HALF * half : HALF * (half + 1)],
+                in_=bank[:].rearrange("p g u b -> p g b u"),
+            )
 
-        def quantise(n, pieces=1):
-            codes = codes_pool.tile([P, UNIT * P], U32, name="codes", align_bytes=256)
-            scales = codes_pool.tile([P, UNIT * P], U8, name="scales", align_bytes=256)
-            width = UNIT * P // pieces
-            for lo in range(0, UNIT * P, width):
-                nc.vector.quantize_mx(
-                    out=codes[:, lo : lo + width].bitcast(FP8X4),
-                    scales=scales[:, lo : lo + width],
-                    in_=grouped_tiles[n][:, PACK * lo : PACK * (lo + width)],
-                )
-            code_tiles[n] = (codes, scales)
-
-        def multiply(n):
-            bt, sb = units[n]
+        def quantise(x):
+            n, half = divmod(x, 2)
+            if half == 0:
+                codes = codes_pool.tile([P, UNIT * P], U32, name="codes", align_bytes=256)
+                scales = codes_pool.tile([P, UNIT * P], U8, name="scales", align_bytes=256)
+                code_tiles[n] = (codes, scales)
             codes, scales = code_tiles[n]
-            if sb == 0:
-                acc[bt] = acc_psum.tile([P, EMBED], F32, name="acc%d" % bt)
-            for i in range(UNIT):
-                g = sb * UNIT + i
+            cols = slice(half * HALF * P, (half + 1) * HALF * P)
+            nc.vector.quantize_mx(
+                out=codes[:, cols].bitcast(FP8X4),
+                scales=scales[:, cols],
+                in_=grouped_tiles[n][:, half * HALF * K_PASS : (half + 1) * HALF * K_PASS],
+            )
+
+        def multiply(x):
+            n, half = divmod(x, 2)
+            codes, scales = code_tiles[n]
+            for i in range(HALF * half, HALF * (half + 1)):
+                bt, g = units[n][i]
+                if g == 0:
+                    acc[bt] = acc_psum.tile([P, EMBED], F32, name="acc%d" % bt)
                 cols = slice(i * P, (i + 1) * P)
                 nc.tensor.matmul_mx(
                     out=acc[bt][:],
                     lhsT=codes[:, cols].bitcast(FP8X4),
                     lhsT_scale=scales[:, cols],
                     rhs=w2_codes[:, g, :].bitcast(FP8X4),
-                    rhs_scale=w2_planes[4 * i : P, sb, :],
+                    rhs_scale=w2_planes[4 * (g % UNIT) : P, g // UNIT, :],
                     start=(g == 0),
                     stop=(g == PASSES - 1),
                 )
@@ -448,9 +463,8 @@ def tile_hotpatchcapsmodel_pa_k_kernel(
                 )
 
         ending = [
-            ((add_bias,), (rectify,)),
-            ((negate_mean,), (square, root)),
-            ((norm,), ()),
+            ((add_bias,), (rectify, square, root)),
+            ((negate_mean, norm), ()),
             ((flip_norm,), (gain_and_shift,)),
             ((group_h, quantise_h), ()),
             ((multiply_h,), ()),
@@ -459,86 +473,99 @@ def tile_hotpatchcapsmodel_pa_k_kernel(
             ((cap_norm, cap_shift), ()),
         ]
 
-        nc.vector.memset(w2_planes[:, 0, :].bitcast(I32), 0)
-        nc.vector.memset(eps_col[:], EPS)
-        nc.vector.memset(vec_rows[:].bitcast(I32), 0)
-        nc.vector.memset(w2_planes[:, 1:GROUPS, :].bitcast(I32), 0)
-        nc.scalar.activation(out=table_warm[:], in_=eps_col[:], func=ACT.Abs_reciprocal_sqrt)
-        make_identity(nc, ident_f32[:])
-        make_identity(nc, ident_bf[:])
+        with tc.manual_schedule():
+            nc.vector.memset(w2_planes[:, 0, :].bitcast(I32), 0)
+            nc.vector.memset(eps_col[:], EPS)
+            nc.vector.memset(vec_rows[:].bitcast(I32), 0)
+            nc.vector.memset(w2_planes[:, 1:GROUPS, :].bitcast(I32), 0)
+            nc.scalar.activation(out=table_warm[:], in_=eps_col[:], func=ACT.Abs_reciprocal_sqrt)
+            make_identity(nc, ident_f32[:])
+            make_identity(nc, ident_bf[:])
 
-        load_h1(0, pieces=2)
-        load_scales(0)
-        load_w2(0, 2)
-        load_w2(2, 2)
-        load_h1(1)
-        load_h1(2)
-        load_h1(3)
-        load_small()
-        next_w2 = UNIT
-        next_h1 = 4
+            load_h1(0, apart=True)
+            load_scales(0)
+            loaded_pairs = {0}
+            loaded_scales = {0}
+            load_w2(0)
+            loaded_h1 = [1]
 
-        sort(0, pieces=2)
-        flip(0)
-        quantise(0, pieces=2)
-        multiply(0)
-        sort(1)
-        flip(1)
-        sort(2)
+            def load_up_to(n):
+                while loaded_h1[0] < min(n, n_units):
+                    load_h1(loaded_h1[0])
+                    for bt, g in units[loaded_h1[0]]:
+                        if g // UNIT not in loaded_scales:
+                            loaded_scales.add(g // UNIT)
+                            load_scales(g // UNIT)
+                        if g // HALF not in loaded_pairs:
+                            loaded_pairs.add(g // HALF)
+                            load_w2(g // HALF)
+                    loaded_h1[0] += 1
 
-        prepare = {1: (sort_pcw,), 2: (flip_pcw,), 3: (quantise_pcw,), 7: (flip_gains,)}
-        prepare[8] = (lambda: spread_rows(ROW_B2, 8, AT_B2),)
-        prepare[9] = (lambda: spread_rows(ROW_PC + 4, 2, AT_PC_BETA), centre_bias)
-        active = []
+            load_up_to(4)
+            load_small()
 
-        def advance(part):
-            now = [(bt, steps[0][part]) for bt, steps in reversed(active) if steps]
-            for i in range(max([len(fs) for bt, fs in now], default=0)):
-                for bt, fs in now:
-                    if i < len(fs):
-                        fs[i](bt)
+            sort(0, pieces=2)
+            flip(0)
+            flip(1)
+            quantise(0)
+            quantise(1)
+            multiply(0)
+            multiply(1)
+            sort(1)
+            flip(2)
+            flip(3)
+            sort(2)
 
-        def drop():
+            prepare = {1: (sort_pcw,), 2: (flip_pcw,), 3: (quantise_pcw,), 7: (flip_gains,)}
+            prepare[8] = (lambda: spread_rows(ROW_B2, 8, AT_B2),)
+            prepare[9] = (lambda: spread_rows(ROW_PC + 4, 2, AT_PC_BETA), centre_bias)
+            active = []
+            flipped = [4]
+            sorted_units = [3]
+            quantised = [2]
+
+            def advance(part):
+                now = [(bt, steps[0][part]) for bt, steps in reversed(active) if steps]
+                for i in range(max([len(fs) for bt, fs in now], default=0)):
+                    for bt, fs in now:
+                        if i < len(fs):
+                            fs[i](bt)
+
+            def target(x):
+                if 12 <= x < 63:
+                    return x + 6 - (x - 12) % 3
+                return 2 * (x // 2) + 4
+
+            for x in range(2 * n_units):
+                n, half = divmod(x, 2)
+                load_up_to(n + LOAD_AHEAD)
+                before = flipped[0]
+                if n > 0:
+                    multiply(x)
+                while quantised[0] < min(before, x + 4):
+                    quantise(quantised[0])
+                    quantised[0] += 1
+                while flipped[0] < min(target(x + 1), 2 * n_units):
+                    flip(flipped[0])
+                    flipped[0] += 1
+                while sorted_units[0] < min((target(x + 3) + 1) // 2, n_units):
+                    sort(sorted_units[0])
+                    sorted_units[0] += 1
+                if half == 1:
+                    for f in prepare.get(n, ()):
+                        f()
+                if n < n_units - 1 and half == 1:
+                    advance(0)
+                    advance(1)
+                    for bt, steps in active:
+                        if steps:
+                            steps.remove(steps[0])
+                if half == 1:
+                    if units[n][-1][1] == PASSES - 1:
+                        active.append((units[n][-1][0], list(ending)))
+        while any(steps for bt, steps in active):
+            advance(0)
+            advance(1)
             for bt, steps in active:
                 if steps:
                     steps.remove(steps[0])
-
-        loaded = [next_h1, next_w2]
-
-        def step(n):
-            while loaded[0] < min(n + LOAD_AHEAD, n_units):
-                sb = units[loaded[0]][1]
-                load_h1(loaded[0])
-                loaded[0] += 1
-                if sb * UNIT >= loaded[1]:
-                    load_scales(sb)
-                    load_w2(loaded[1], UNIT // 2)
-                    load_w2(loaded[1] + UNIT // 2, UNIT // 2)
-                    loaded[1] += UNIT
-            if n > 0:
-                multiply(n)
-            if n + 1 < n_units:
-                quantise(n + 1)
-            if n + 2 < n_units:
-                flip(n + 2)
-            if n + 3 < n_units:
-                sort(n + 3)
-            for f in prepare.get(n, ()):
-                f()
-            if n < n_units - 1:
-                advance(0)
-                advance(1)
-                drop()
-            if units[n][1] == GROUPS - 1:
-                active.append((units[n][0], list(ending)))
-
-        for n in range(n_units):
-            step(n)
-        rest = []
-        for bt, steps in reversed(active):
-            rest.append([(f, bt) for vector_part, scalar_part in steps for f in vector_part + scalar_part])
-        while any(rest):
-            for fs in rest:
-                for f, bt in fs[:1]:
-                    f(bt)
-                    fs.remove((f, bt))

@@ -532,8 +532,8 @@ def tile_hotpatchcapsmodel_pa_k_kernel(
                             fs[i](bt)
 
             def target(x):
-                if 12 <= x < 63:
-                    return x + 6 - (x - 12) % 3
+                if 99 <= x < 99:
+                    return x + 6 - (x - 99) % 3
                 return 2 * (x // 2) + 4
 
             for x in range(2 * n_units):

@@ -65,8 +65,8 @@ def tile_hotpatchcapsmodel_pa_k_kernel(
         raw_pool = ctx.enter_context(tc.tile_pool(name="raw", bufs=12))
         stage = ctx.enter_context(tc.tile_pool(name="stage", bufs=4))
         codes_pool = ctx.enter_context(tc.tile_pool(name="codes", bufs=6))
-        work = ctx.enter_context(tc.tile_pool(name="work", bufs=2))
-        small = ctx.enter_context(tc.tile_pool(name="small", bufs=2))
+        work = ctx.enter_context(tc.tile_pool(name="work", bufs=4))
+        small = ctx.enter_context(tc.tile_pool(name="small", bufs=4))
         flip_psum = ctx.enter_context(tc.psum_pool(name="flip", bufs=4))
         acc_psum = ctx.enter_context(tc.psum_pool(name="acc", bufs=1))
 
@@ -269,10 +269,9 @@ def tile_hotpatchcapsmodel_pa_k_kernel(
             nc.vector.tensor_scalar_mul(out=neg_mean[:], in0=t["z_sum", bt][:], scalar1=-1.0 / EMBED)
 
         def square(bt):
-            squares = new(bt, work, [P, EMBED], F32, "squares")
             sq_sum = new(bt, small, [P, 1], F32, "sq_sum")
             nc.scalar.activation(
-                out=squares[:],
+                out=t["biased", bt][:],
                 in_=t["z", bt][:],
                 func=ACT.Square,
                 scale=-float(EMBED),
@@ -291,9 +290,8 @@ def tile_hotpatchcapsmodel_pa_k_kernel(
             )
 
         def norm(bt):
-            normed = new(bt, work, [P, EMBED], F32, "normed_z")
             nc.vector.tensor_scalar(
-                out=normed[:],
+                out=t["biased", bt][:],
                 in0=t["z", bt][:],
                 scalar1=t["neg_mean", bt][:],
                 scalar2=t["rstd", bt][:],
@@ -305,7 +303,7 @@ def tile_hotpatchcapsmodel_pa_k_kernel(
             h_flip = new(bt, acc_psum, [P, PACK, P], F32, "h_flip", tag="acc%d" % bt)
             for i in range(PACK):
                 nc.tensor.transpose(
-                    h_flip[:, i, :], t["normed_z", bt][:, i * P : (i + 1) * P], ident_f32[:]
+                    h_flip[:, i, :], t["biased", bt][:, i * P : (i + 1) * P], ident_f32[:]
                 )
 
         def gain_and_shift(bt):
@@ -467,8 +465,8 @@ def tile_hotpatchcapsmodel_pa_k_kernel(
             ((negate_mean, norm), ()),
             ((flip_norm,), (gain_and_shift,)),
             ((group_h, quantise_h), ()),
-            ((multiply_h,), ()),
-            ((cap_sum, cap_bias, cap_centre), (cap_square,)),
+            ((multiply_h, cap_sum, cap_bias), ()),
+            ((cap_centre,), (cap_square,)),
             ((cap_gain, cap_square_sum), (cap_root,)),
             ((cap_norm, cap_shift), ()),
         ]
@@ -532,8 +530,6 @@ def tile_hotpatchcapsmodel_pa_k_kernel(
                             fs[i](bt)
 
             def target(x):
-                if 99 <= x < 99:
-                    return x + 6 - (x - 99) % 3
                 return 2 * (x // 2) + 4
 
             for x in range(2 * n_units):
@@ -554,15 +550,14 @@ def tile_hotpatchcapsmodel_pa_k_kernel(
                 if half == 1:
                     for f in prepare.get(n, ()):
                         f()
+                if half == 1 and units[n][-1][1] == PASSES - 1:
+                    active.append((units[n][-1][0], list(ending)))
                 if n < n_units - 1 and half == 1:
                     advance(0)
                     advance(1)
                     for bt, steps in active:
                         if steps:
                             steps.remove(steps[0])
-                if half == 1:
-                    if units[n][-1][1] == PASSES - 1:
-                        active.append((units[n][-1][0], list(ending)))
         while any(steps for bt, steps in active):
             advance(0)
             advance(1)

@@ -253,6 +253,17 @@ def tile_hotpatchcapsmodel_pa_k_kernel(
             t[what, bt] = pool.tile(shape, dtype, name=what, **kw)
             return t[what, bt]
 
+        def keep_warm(bt, what):
+            if bt == B_TILES - 1:
+                idle = flip_psum.tile([P, EMBED // 2], F32, name="idle", tag="flip")
+                nc.tensor.matmul(
+                    out=idle[:],
+                    lhsT=ident_f32[:],
+                    rhs=t[what, bt][:, 0 : EMBED // 2],
+                    start=True,
+                    stop=True,
+                )
+
         def add_bias(bt):
             biased = new(bt, work, [P, EMBED], F32, "biased")
             nc.vector.tensor_tensor(
@@ -460,8 +471,11 @@ def tile_hotpatchcapsmodel_pa_k_kernel(
                     in_=result[:, columns(part)],
                 )
 
+        def warm_on_z(bt):
+            keep_warm(bt, "z")
+
         ending = [
-            ((add_bias,), (rectify, square, root)),
+            ((add_bias,), (rectify, warm_on_z, square, root)),
             ((negate_mean, norm), ()),
             ((flip_norm,), (gain_and_shift,)),
             ((group_h, quantise_h), ()),
@@ -486,17 +500,24 @@ def tile_hotpatchcapsmodel_pa_k_kernel(
             loaded_scales = {0}
             load_w2(0)
             loaded_h1 = [1]
+            late = []
 
             def load_up_to(n):
                 while loaded_h1[0] < min(n, n_units):
                     load_h1(loaded_h1[0])
+                    for pair in late:
+                        load_w2(pair)
+                    late.clear()
                     for bt, g in units[loaded_h1[0]]:
                         if g // UNIT not in loaded_scales:
                             loaded_scales.add(g // UNIT)
                             load_scales(g // UNIT)
                         if g // HALF not in loaded_pairs:
                             loaded_pairs.add(g // HALF)
-                            load_w2(g // HALF)
+                            if g % UNIT < HALF or units[loaded_h1[0]][0][0] != units[loaded_h1[0]][-1][0]:
+                                load_w2(g // HALF)
+                            else:
+                                late.append(g // HALF)
                     loaded_h1[0] += 1
 
             load_up_to(4)

from contextlib import ExitStack

import concourse.mybir as mybir
from concourse.masks import make_identity

F32 = mybir.dt.float32
BF16 = mybir.dt.bfloat16
I32 = mybir.dt.int32
U32 = mybir.dt.uint32
U8 = mybir.dt.uint8
FP8X4 = mybir.dt.float8_e4m3fn_x4
ALU = mybir.AluOpType
ACT = mybir.ActivationFunctionType
AX = mybir.AxisListType

P = 128
PACK = 4
K_PASS = P * PACK
BATCH = 512
HIDDEN = 16384
EMBED = 512
CAPSULES = 32
CAP_DIM = 8
CAP_OUT = CAPSULES * CAP_DIM
EPS = 1e-5

B_TILES = BATCH // P
PASSES = HIDDEN // K_PASS
UNIT = 4
HALF = 2
UNIT_K = UNIT * K_PASS
GROUPS = PASSES // UNIT
LOAD_AHEAD = 9

FLOPS = 2 * BATCH * HIDDEN * EMBED + 2 * BATCH * EMBED * CAP_OUT

ROW_GAIN = 0
ROW_SHIFT = 4
ROW_B2 = 8
ROW_PC = 12
AT_B2 = 0
AT_PC_B = EMBED
AT_PC_G = EMBED + CAP_OUT
AT_PC_BETA = EMBED + 2 * CAP_OUT
SPREAD = EMBED + 3 * CAP_OUT


def tile_hotpatchcapsmodel_pa_k_kernel(
    tc, h1, W2_words, W2_scales, b2, ln_g, ln_b, pc_W, pc_b, pc_g, pc_beta, out
):
    nc = tc.nc
    def alone(bt, sb):
        return [(bt, sb * UNIT + i) for i in range(UNIT)]

    def in_pairs(bt, pair):
        return [(b, pair * HALF + i) for b in (bt, bt + 1) for i in range(HALF)]

    units = [in_pairs(bt, pair) for pair in range(2) for bt in range(0, B_TILES, 2)]
    units += [alone(bt, sb) for sb in range(2 // 2, 5) for bt in range(B_TILES)]
    units += [alone(bt, sb) for bt, sb in ((0, 5), (1, 5), (0, 6), (1, 6), (0, 7), (1, 7), (2, 5), (2, 6), (2, 7), (3, 5), (3, 6), (3, 7))]
    n_units = len(units)

    with ExitStack() as ctx:
        const = ctx.enter_context(tc.tile_pool(name="const", bufs=1))
        raw_pool = ctx.enter_context(tc.tile_pool(name="raw", bufs=12))
        stage = ctx.enter_context(tc.tile_pool(name="stage", bufs=4))
        codes_pool = ctx.enter_context(tc.tile_pool(name="codes", bufs=6))
        work = ctx.enter_context(tc.tile_pool(name="work", bufs=4))
        small = ctx.enter_context(tc.tile_pool(name="small", bufs=4))
        flip_psum = ctx.enter_context(tc.psum_pool(name="flip", bufs=4))
        acc_psum = ctx.enter_context(tc.psum_pool(name="acc", bufs=1))

        w2_codes = const.tile([P, PASSES, EMBED], U32, align_bytes=256)
        w2_planes = const.tile([P, GROUPS, EMBED], U8, align_bytes=256)
        vec_rows = const.tile([P, P], BF16)
        pcw_raw = const.tile([P, P * CAP_DIM], BF16)
        eps_col = const.tile([P, 1], F32)
        table_warm = const.tile([P, 1], F32)
        ident_f32 = const.tile([P, P], F32, align_bytes=256)
        ident_bf = const.tile([P, P], BF16)

        raw_tiles = {}
        sorted_tiles = {}
        grouped_tiles = {}
        code_tiles = {}
        acc = {}

        def load_h1(n, apart=False):
            slots = units[n]
            raw = raw_pool.tile([P, UNIT_K], BF16, name="raw", align_bytes=256)
            bt, g = slots[0]
            tiles = 1 + slots[-1][0] - bt
            passes = UNIT // tiles
            if tiles == 1 or not apart:
                nc.sync.dma_start(
                    out=raw[:].rearrange("p (t k) -> p t k", t=tiles),
                    in_=h1.rearrange("(t p) k -> p t k", p=P)[
                        :, bt : bt + tiles, g * K_PASS : (g + passes) * K_PASS
                    ],
                )
            else:
                for i in range(tiles):
                    nc.sync.dma_start(
                        out=raw[:, i * passes * K_PASS : (i + 1) * passes * K_PASS],
                        in_=h1[(bt + i) * P : (bt + i + 1) * P, g * K_PASS : (g + passes) * K_PASS],
                    )
            raw_tiles[n] = raw

        def load_w2(pair):
            passes = slice(HALF * pair, HALF * (pair + 1))
            nc.sync.dma_start(
                out=w2_codes[:, passes, :].bitcast(I32),
                in_=W2_words[passes].rearrange("g p n t -> p g (n t)").bitcast(I32),
            )

        def load_scales(sb):
            for quadrant in range(4):
                nc.sync.dma_start(
                    out=w2_planes[32 * quadrant : 32 * quadrant + 4 * UNIT, sb, :].bitcast(I32),
                    in_=W2_scales[sb * UNIT : (sb + 1) * UNIT, 4 * quadrant : 4 * quadrant + 4, :].bitcast(I32),
                )

        def load_small():
            nc.gpsimd.dma_start(out=pcw_raw[:], in_=pc_W.rearrange("n (a e) p -> (n a) (e p)", e=P))
            for vec, row in ((b2, ROW_B2), (ln_g, ROW_GAIN), (ln_b, ROW_SHIFT)):
                nc.gpsimd.dma_start(out=vec_rows[row : row + 4, :], in_=vec.rearrange("(r e) -> r e", e=P))
            for i, vec in enumerate((pc_b, pc_g, pc_beta)):
                nc.gpsimd.dma_start(
                    out=vec_rows[ROW_PC + 2 * i : ROW_PC + 2 * i + 2, :],
                    in_=vec.rearrange("(r n) p -> r (n p)", r=2),
                )

        def sort(n, pieces=1):
            words = raw_tiles[n][:].bitcast(F32)
            by_parity = words.rearrange("b (g j u) -> b g u j", g=UNIT, u=2)
            sorted_words = stage.tile([P, UNIT, 2, P], F32, name="sorted_words", align_bytes=256)
            step = UNIT // pieces
            for lo in range(0, UNIT, step):
                nc.vector.tensor_copy(
                    out=sorted_words[:, lo : lo + step], in_=by_parity[:, lo : lo + step]
                )
            sorted_tiles[n] = sorted_words

        def flip(x):
            n, half = divmod(x, 2)
            if half == 0:
                grouped_tiles[n] = stage.tile([P, UNIT_K], BF16, name="grouped", align_bytes=256)
            grouped_words = grouped_tiles[n][:].bitcast(F32).rearrange("p (g b u) -> p g b u", g=UNIT, u=2)
            bank = flip_psum.tile([P, HALF, 2, P], F32, name="bank", tag="flip")
            for i in range(HALF):
                for u in range(2):
                    nc.tensor.transpose(
                        bank[:, i, u, :], sorted_tiles[n][:, HALF * half + i, u, :], ident_f32[:]
                    )
            nc.scalar.copy(
                out=grouped_words[:, HALF * half : HALF * (half + 1)],
                in_=bank[:].rearrange("p g u b -> p g b u"),
            )

        def quantise(x):
            n, half = divmod(x, 2)
            if half == 0:
                codes = codes_pool.tile([P, UNIT * P], U32, name="codes", align_bytes=256)
                scales = codes_pool.tile([P, UNIT * P], U8, name="scales", align_bytes=256)
                code_tiles[n] = (codes, scales)
            codes, scales = code_tiles[n]
            cols = slice(half * HALF * P, (half + 1) * HALF * P)
            nc.vector.quantize_mx(
                out=codes[:, cols].bitcast(FP8X4),
                scales=scales[:, cols],
                in_=grouped_tiles[n][:, half * HALF * K_PASS : (half + 1) * HALF * K_PASS],
            )

        def multiply(x):
            n, half = divmod(x, 2)
            codes, scales = code_tiles[n]
            for i in range(HALF * half, HALF * (half + 1)):
                bt, g = units[n][i]
                if g == 0:
                    acc[bt] = acc_psum.tile([P, EMBED], F32, name="acc%d" % bt)
                cols = slice(i * P, (i + 1) * P)
                nc.tensor.matmul_mx(
                    out=acc[bt][:],
                    lhsT=codes[:, cols].bitcast(FP8X4),
                    lhsT_scale=scales[:, cols],
                    rhs=w2_codes[:, g, :].bitcast(FP8X4),
                    rhs_scale=w2_planes[4 * (g % UNIT) : P, g // UNIT, :],
                    start=(g == 0),
                    stop=(g == PASSES - 1),
                )

        spread = const.tile([P, SPREAD], BF16)
        gain_shift = const.tile([P, 8], F32)
        bias_sum = const.tile([P, CAPSULES], F32)
        centred_bias = const.tile([P, CAP_OUT], F32)
        pcw_sorted = const.tile([P, CAP_DIM, P], BF16)
        pcw_grouped = const.tile([P, CAPSULES, CAP_DIM, PACK], BF16, align_bytes=64)
        pcw_codes = const.tile([P, CAP_OUT], U32, align_bytes=64)
        pcw_scales = const.tile([P, CAP_OUT], U8, align_bytes=64)

        def spread_rows(first, count, at):
            rep = flip_psum.tile([P, count * P], BF16, name="rep", tag="flip")
            for r in range(count):
                nc.tensor.matmul(
                    out=rep[:, r * P : (r + 1) * P],
                    lhsT=ident_bf[:, first + r : first + r + 1].to_broadcast([P, P]),
                    rhs=vec_rows[:],
                    start=True,
                    stop=True,
                )
            nc.scalar.copy(out=spread[:, at : at + count * P], in_=rep[:])

        def centre_bias():
            bias = spread[:, AT_PC_B : AT_PC_B + CAP_OUT].rearrange("b (n p) -> b n p", p=CAP_DIM)
            nc.vector.reduce_sum(out=bias_sum[:], in_=bias, axis=AX.X)
            nc.vector.scalar_tensor_tensor(
                out=centred_bias[:].rearrange("b (n p) -> b n p", p=CAP_DIM),
                in0=bias_sum[:].unsqueeze(2).to_broadcast([P, CAPSULES, CAP_DIM]),
                scalar=-1.0 / CAP_DIM,
                in1=bias,
                op0=ALU.mult,
                op1=ALU.add,
            )

        def flip_gains():
            rep = flip_psum.tile([P, P], BF16, name="rep", tag="flip")
            nc.tensor.transpose(rep[:], vec_rows[:], ident_bf[:])
            nc.scalar.copy(out=gain_shift[:], in_=rep[:, ROW_GAIN : ROW_SHIFT + 4])

        def sort_pcw():
            nc.vector.tensor_copy(
                out=pcw_sorted[:], in_=pcw_raw[:].rearrange("q (e p) -> q p e", p=CAP_DIM)
            )

        def flip_pcw():
            pcw_flip = flip_psum.tile([P, CAP_DIM, P], BF16, name="pcw_flip", tag="flip")
            for p in range(CAP_DIM):
                nc.tensor.transpose(pcw_flip[:, p, :], pcw_sorted[:, p, :], ident_bf[:])
            nc.scalar.copy(
                out=pcw_grouped[:], in_=pcw_flip[:].rearrange("e p (n a) -> e n p a", a=PACK)
            )

        def quantise_pcw():
            nc.vector.quantize_mx(
                out=pcw_codes[:].bitcast(FP8X4),
                scales=pcw_scales[:],
                in_=pcw_grouped[:].rearrange("e n p a -> e (n p a)"),
            )

        t = {}

        def new(bt, pool, shape, dtype, what, **kw):
            t[what, bt] = pool.tile(shape, dtype, name=what, **kw)
            return t[what, bt]

        def keep_warm(bt, what):
            if bt == B_TILES - 1:
                idle = flip_psum.tile([P, EMBED // 2], F32, name="idle", tag="flip")
                nc.tensor.matmul(
                    out=idle[:],
                    lhsT=ident_f32[:],
                    rhs=t[what, bt][:, 0 : EMBED // 2],
                    start=True,
                    stop=True,
                )

        def add_bias(bt):
            biased = new(bt, work, [P, EMBED], F32, "biased")
            nc.vector.tensor_tensor(
                out=biased[:], in0=acc[bt][:], in1=spread[:, AT_B2 : AT_B2 + EMBED], op=ALU.add
            )

        def rectify(bt):
            z = new(bt, work, [P, EMBED], F32, "z")
            z_sum = new(bt, small, [P, 1], F32, "z_sum")
            nc.scalar.activation(out=z[:], in_=t["biased", bt][:], func=ACT.Relu, accum_out=z_sum[:])

        def negate_mean(bt):
            neg_mean = new(bt, small, [P, 1], F32, "neg_mean")
            nc.vector.tensor_scalar_mul(out=neg_mean[:], in0=t["z_sum", bt][:], scalar1=-1.0 / EMBED)

        def square(bt):
            sq_sum = new(bt, small, [P, 1], F32, "sq_sum")
            nc.scalar.activation(
                out=t["biased", bt][:],
                in_=t["z", bt][:],
                func=ACT.Square,
                scale=-float(EMBED),
                bias=t["z_sum", bt][:],
                accum_out=sq_sum[:],
            )

        def root(bt):
            rstd = new(bt, small, [P, 1], F32, "rstd")
            nc.scalar.activation(
                out=rstd[:],
                in_=t["sq_sum", bt][:],
                func=ACT.Abs_reciprocal_sqrt,
                scale=1.0 / EMBED**3,
                bias=eps_col[:],
            )

        def norm(bt):
            nc.vector.tensor_scalar(
                out=t["biased", bt][:],
                in0=t["z", bt][:],
                scalar1=t["neg_mean", bt][:],
                scalar2=t["rstd", bt][:],
                op0=ALU.add,
                op1=ALU.mult,
            )

        def flip_norm(bt):
            h_flip = new(bt, acc_psum, [P, PACK, P], F32, "h_flip", tag="acc%d" % bt)
            for i in range(PACK):
                nc.tensor.transpose(
                    h_flip[:, i, :], t["biased", bt][:, i * P : (i + 1) * P], ident_f32[:]
                )

        def gain_and_shift(bt):
            h = new(bt, work, [P, PACK, P], BF16, "h")
            by_vector = PACK // 2 if bt == B_TILES - 1 else 0
            for i in range(PACK):
                gain = gain_shift[:, ROW_GAIN + i : ROW_GAIN + i + 1]
                shift = gain_shift[:, ROW_SHIFT + i : ROW_SHIFT + i + 1]
                if i >= PACK - by_vector:
                    nc.vector.tensor_scalar(
                        out=h[:, i, :],
                        in0=t["h_flip", bt][:, i, :],
                        scalar1=gain,
                        scalar2=shift,
                        op0=ALU.mult,
                        op1=ALU.add,
                    )
                else:
                    nc.scalar.activation(
                        out=h[:, i, :],
                        in_=t["h_flip", bt][:, i, :],
                        func=ACT.Identity,
                        scale=gain,
                        bias=shift,
                    )

        def group_h(bt):
            h_grouped = new(bt, work, [P, P, PACK], BF16, "h_grouped", align_bytes=64)
            nc.vector.tensor_copy(out=h_grouped[:], in_=t["h", bt][:].rearrange("e i b -> e b i"))

        def quantise_h(bt):
            h_codes = new(bt, work, [P, P], U32, "h_codes", align_bytes=64)
            h_scales = new(bt, work, [P, P], U8, "h_scales", align_bytes=64)
            nc.vector.quantize_mx(
                out=h_codes[:].bitcast(FP8X4),
                scales=h_scales[:],
                in_=t["h_grouped", bt][:].rearrange("e b i -> e (b i)"),
            )

        def multiply_h(bt):
            prim = new(bt, acc_psum, [P, CAP_OUT], F32, "prim", tag="acc%d" % bt)
            nc.tensor.matmul_mx(
                out=prim[:],
                lhsT=t["h_codes", bt][:].bitcast(FP8X4),
                lhsT_scale=t["h_scales", bt][:],
                rhs=pcw_codes[:].bitcast(FP8X4),
                rhs_scale=pcw_scales[:],
                start=True,
                stop=True,
            )

        by_capsule = [P, CAPSULES, CAP_DIM]

        def flat(ap):
            return ap.rearrange("b n p -> b (n p)")

        def parts(bt):
            half = CAPSULES // 2
            return (slice(0, half), slice(half, CAPSULES)) if bt == B_TILES - 1 else (slice(0, CAPSULES),)

        def columns(part):
            return slice(part.start * CAP_DIM, part.stop * CAP_DIM)

        def cap_bias(bt):
            x = new(bt, work, by_capsule, F32, "x")
            for part in parts(bt):
                nc.vector.tensor_tensor(
                    out=flat(x[:, part]),
                    in0=t["prim", bt][:, columns(part)],
                    in1=centred_bias[:, columns(part)],
                    op=ALU.add,
                )

        def cap_sum(bt):
            x_sum = new(bt, small, [P, CAPSULES], F32, "x_sum")
            for part in parts(bt):
                nc.vector.reduce_sum(
                    out=x_sum[:, part],
                    in_=t["prim", bt][:, columns(part)].rearrange("b (n p) -> b n p", p=CAP_DIM),
                    axis=AX.X,
                )

        def cap_centre(bt):
            centred = new(bt, work, by_capsule, F32, "centred")
            for part in parts(bt):
                shape = [P, part.stop - part.start, CAP_DIM]
                nc.vector.scalar_tensor_tensor(
                    out=centred[:, part],
                    in0=t["x_sum", bt][:, part].unsqueeze(2).to_broadcast(shape),
                    scalar=-1.0 / CAP_DIM,
                    in1=t["x", bt][:, part],
                    op0=ALU.mult,
                    op1=ALU.add,
                )

        def cap_square(bt):
            cap_squares = new(bt, work, by_capsule, F32, "cap_squares")
            for part in parts(bt):
                nc.scalar.activation(
                    out=cap_squares[:, part], in_=t["centred", bt][:, part], func=ACT.Square
                )

        def cap_gain(bt):
            gained = new(bt, work, by_capsule, F32, "cap_gained")
            for part in parts(bt):
                nc.vector.tensor_tensor(
                    out=flat(gained[:, part]),
                    in0=flat(t["centred", bt][:, part]),
                    in1=spread[:, AT_PC_G : AT_PC_G + CAP_OUT][:, columns(part)],
                    op=ALU.mult,
                )

        def cap_square_sum(bt):
            cap_sq_sum = new(bt, small, [P, CAPSULES], F32, "cap_sq_sum")
            for part in parts(bt):
                nc.vector.reduce_sum(
                    out=cap_sq_sum[:, part], in_=t["cap_squares", bt][:, part], axis=AX.X
                )

        def cap_root(bt):
            cap_rstd = new(bt, small, [P, CAPSULES], F32, "cap_rstd")
            for part in parts(bt):
                nc.scalar.activation(
                    out=cap_rstd[:, part],
                    in_=t["cap_sq_sum", bt][:, part],
                    func=ACT.Abs_reciprocal_sqrt,
                    scale=1.0 / CAP_DIM,
                    bias=eps_col[:],
                )

        def cap_norm(bt):
            normed = new(bt, work, by_capsule, F32, "normed")
            for part in parts(bt):
                shape = [P, part.stop - part.start, CAP_DIM]
                nc.vector.tensor_tensor(
                    out=normed[:, part],
                    in0=t["cap_gained", bt][:, part],
                    in1=t["cap_rstd", bt][:, part].unsqueeze(2).to_broadcast(shape),
                    op=ALU.mult,
                )

        def cap_shift(bt):
            result = new(bt, work, [P, CAP_OUT], F32, "result")
            for part in parts(bt):
                nc.vector.tensor_tensor(
                    out=result[:, columns(part)],
                    in0=flat(t["normed", bt][:, part]),
                    in1=spread[:, AT_PC_BETA : AT_PC_BETA + CAP_OUT][:, columns(part)],
                    op=ALU.add,
                )
            for part in parts(bt):
                nc.sync.dma_start(
                    out=out[bt * P : (bt + 1) * P, part].rearrange("b n p -> b (n p)"),
                    in_=result[:, columns(part)],
                )

        def warm_on_z(bt):
            keep_warm(bt, "z")

        ending = [
            ((add_bias,), (rectify, warm_on_z, square, root)),
            ((negate_mean, norm), ()),
            ((flip_norm,), (gain_and_shift,)),
            ((group_h, quantise_h), ()),
            ((multiply_h, cap_sum, cap_bias), ()),
            ((cap_centre,), (cap_square,)),
            ((cap_gain, cap_square_sum), (cap_root,)),
            ((cap_norm, cap_shift), ()),
        ]

        with tc.manual_schedule():
            nc.vector.memset(w2_planes[:, 0, :].bitcast(I32), 0)
            nc.vector.memset(eps_col[:], EPS)
            nc.vector.memset(vec_rows[:].bitcast(I32), 0)
            nc.vector.memset(w2_planes[:, 1:GROUPS, :].bitcast(I32), 0)
            nc.scalar.activation(out=table_warm[:], in_=eps_col[:], func=ACT.Abs_reciprocal_sqrt)
            make_identity(nc, ident_f32[:])
            make_identity(nc, ident_bf[:])

            load_h1(0, apart=True)
            load_scales(0)
            loaded_pairs = {0}
            loaded_scales = {0}
            load_w2(0)
            loaded_h1 = [1]
            late = []

            def load_up_to(n):
                while loaded_h1[0] < min(n, n_units):
                    load_h1(loaded_h1[0])
                    for pair in late:
                        load_w2(pair)
                    late.clear()
                    for bt, g in units[loaded_h1[0]]:
                        if g // UNIT not in loaded_scales:
                            loaded_scales.add(g // UNIT)
                            load_scales(g // UNIT)
                        if g // HALF not in loaded_pairs:
                            loaded_pairs.add(g // HALF)
                            if g % UNIT < HALF or units[loaded_h1[0]][0][0] != units[loaded_h1[0]][-1][0]:
                                load_w2(g // HALF)
                            else:
                                late.append(g // HALF)
                    loaded_h1[0] += 1

            load_up_to(4)
            load_small()

            sort(0, pieces=2)
            flip(0)
            flip(1)
            quantise(0)
            quantise(1)
            multiply(0)
            multiply(1)
            sort(1)
            flip(2)
            flip(3)
            sort(2)

            prepare = {1: (sort_pcw,), 2: (flip_pcw,), 3: (quantise_pcw,), 7: (flip_gains,)}
            prepare[8] = (lambda: spread_rows(ROW_B2, 8, AT_B2),)
            prepare[9] = (lambda: spread_rows(ROW_PC + 4, 2, AT_PC_BETA), centre_bias)
            active = []
            flipped = [4]
            sorted_units = [3]
            quantised = [2]

            def advance(part):
                now = [(bt, steps[0][part]) for bt, steps in reversed(active) if steps]
                for i in range(max([len(fs) for bt, fs in now], default=0)):
                    for bt, fs in now:
                        if i < len(fs):
                            fs[i](bt)

            def target(x):
                return 2 * (x // 2) + 4

            for x in range(2 * n_units):
                n, half = divmod(x, 2)
                load_up_to(n + LOAD_AHEAD)
                before = flipped[0]
                if n > 0:
                    multiply(x)
                while quantised[0] < min(before, x + 4):
                    quantise(quantised[0])
                    quantised[0] += 1
                while flipped[0] < min(target(x + 1), 2 * n_units):
                    flip(flipped[0])
                    flipped[0] += 1
                while sorted_units[0] < min((target(x + 3) + 1) // 2, n_units):
                    sort(sorted_units[0])
                    sorted_units[0] += 1
                if half == 1:
                    for f in prepare.get(n, ()):
                        f()
                if half == 1 and units[n][-1][1] == PASSES - 1:
                    active.append((units[n][-1][0], list(ending)))
                if n < n_units - 1 and half == 1:
                    advance(0)
                    advance(1)
                    for bt, steps in active:
                        if steps:
                            steps.remove(steps[0])
        while any(steps for bt, steps in active):
            advance(0)
            advance(1)
            for bt, steps in active:
                if steps:
                    steps.remove(steps[0])
